import numpy as np
import ml_dtypes


def mxq(x, axis, fmt="e4m3"):
    dtype, down = {"e4m3": (ml_dtypes.float8_e4m3fn, 7), "e5m2": (ml_dtypes.float8_e5m2, 14)}[fmt]
    v = np.moveaxis(np.asarray(x, np.float32).astype(ml_dtypes.bfloat16).astype(np.float64), axis, -1)
    blocks = v.reshape(v.shape[:-1] + (-1, 32))
    amax = np.abs(blocks).max(-1, keepdims=True)
    byte = np.maximum(np.where(amax > 0, np.frexp(amax)[1] - 1 + 127, 0) - down, 1)
    scale = np.exp2(byte - 127.0)
    codes = (blocks / scale).astype(np.float32).astype(dtype).astype(np.float64)
    return np.moveaxis((codes * scale).reshape(v.shape), -1, axis)


WIDE = False


def mx_kscale(k):
    if not WIDE:
        return np.ones(k)
    levels = np.array([10, -10, 5, -5, 0])
    if k % 512:
        return np.exp2(np.random.permutation(np.resize(levels, k // 32))).repeat(32)
    a = np.empty((k // 512, 16))
    for p in range(k // 512):
        a[p, :8] = np.random.permutation(np.resize(levels, 8))
        for g in range(8):
            far = levels[np.abs(levels - a[p, g]) >= 10]
            a[p, g + 8] = far[np.random.randint(len(far))]
    return np.exp2(a.ravel()).repeat(32)


BF16 = ml_dtypes.bfloat16


def bf(x):
    return np.asarray(x, np.float32).astype(BF16)


def f64(x):
    return np.asarray(x).astype(np.float64)


B, CH, C1, C2, D, NF, W, H = 1, 1024, 128, 512, 2, 8, 16, 16
N = NF * W * H
M = NF * (W // D) * (H // D)


def conv(xq, w, b):
    return (mxq(f64(w), 1, "e4m3") @ xq) + f64(b)[None, :, None]


def maxpool_wh(v):
    return v.reshape(B, -1, NF, W // D, D, H // D, D).max(axis=(4, 6)).reshape(B, -1, M)


def draw0():
    s = mx_kscale(CH)
    return {"x": bf(np.random.standard_normal((B, CH, NF, W, H)) * s[None, :, None, None, None]),
            "w_theta": bf(np.random.standard_normal((C1, CH)) * 0.3 / np.sqrt(CH) / s),
            "b_theta": bf(np.random.standard_normal(C1) * 0.1),
            "w_phi": bf(np.random.standard_normal((C1, CH)) * 0.3 / np.sqrt(CH) / s),
            "b_phi": bf(np.random.standard_normal(C1) * 0.1),
            "w_g": bf(np.random.standard_normal((C2, CH)) / np.sqrt(CH) / s),
            "b_g": bf(np.random.standard_normal(C2) * 0.2)}


def core(x, w_theta, b_theta, w_phi, b_phi, w_g, b_g):
    xq = mxq(f64(x).reshape(B, CH, N), 1, "e4m3")
    theta = np.tanh(conv(xq, w_theta, b_theta)).transpose(0, 2, 1)
    phi = maxpool_wh(np.tanh(conv(xq, w_phi, b_phi))).transpose(0, 2, 1)
    g = maxpool_wh(conv(xq, w_g, b_g)).transpose(0, 2, 1)
    return theta, phi, g


def e4m3fn_bytes(y):
    return np.clip(np.asarray(y, np.float64), -448.0, 448.0).astype(np.float32).astype(ml_dtypes.float8_e4m3fn).view(np.uint8)


def e4m3fn_values(b):
    return np.asarray(b, np.uint8).view(ml_dtypes.float8_e4m3fn).astype(np.float64)


def setup_inputs():
    d = draw0()
    x0 = np.asarray(d['x']).astype(np.float64)
    s = (np.max(np.abs(x0), axis=(0, 2, 3, 4), keepdims=True) / 448.0).astype(np.float32)
    out = {}
    for k, v in d.items():
        if k == 'x':
            out['x_bytes'] = e4m3fn_bytes(x0 / s.astype(np.float64))
            out['x_scale'] = s
        else:
            out[k] = v
    return out


def reference(x_bytes, x_scale, w_theta, b_theta, w_phi, b_phi, w_g, b_g):
    return core(e4m3fn_values(x_bytes) * x_scale.astype(np.float64), w_theta, b_theta, w_phi, b_phi, w_g, b_g)

@@ -1,0 +1,270 @@
+from contextlib import ExitStack
+
+import concourse.mybir as mybir
+from concourse.masks import make_identity
+
+FLOPS = 2 * 1024 * 768 * 2048
+
+F32 = mybir.dt.float32
+BF16 = mybir.dt.bfloat16
+U32 = mybir.dt.uint32
+U8 = mybir.dt.uint8
+FP8 = mybir.dt.float8_e4m3fn
+FP8X4 = mybir.dt.float8_e4m3fn_x4
+ACT = mybir.ActivationFunctionType
+ALU = mybir.AluOpType
+AX = mybir.AxisListType
+
+P = 128
+NCHUNK = 4
+NPASS = 2
+CL = 512
+
+V_WIDEN = ((0, 0),)
+W_COPY_ON_SCALAR = (True, True, True, True, True, True)
+U_COPY_ON_SCALAR = True
+
+
+def tile_selfattention3d_pb_kernel(
+    tc, x_bytes, x_scale, w_theta, b_theta, w_phi, b_phi, w_g, b_g, out_0, out_1, out_2
+):
+    nc = tc.nc
+    with ExitStack() as ctx:
+        keep = ctx.enter_context(tc.tile_pool(name="keep", bufs=1))
+        work = ctx.enter_context(tc.tile_pool(name="work", bufs=2))
+        psum = ctx.enter_context(tc.psum_pool(name="psum", bufs=1))
+
+        xsc = keep.tile([P, 8], F32, name="xsc", tag="xsc")
+        nc.sync.dma_start(
+            out=xsc[:].rearrange("p (g t) -> p g t", g=NPASS),
+            in_=x_scale.rearrange("o k a b c -> (o k a b c)").rearrange("(g p t) -> p g t", g=NPASS, p=P, t=4),
+        )
+        xb = x_bytes[0].rearrange("(g p t) f i j -> g p t (f i j)", g=NPASS, p=P, t=4)
+        xbytes = {}
+
+        def load_x(c, g):
+            tl = keep.tile([P, 4, CL], U8, name="xbytes_%d_%d" % (c, g), tag="xbytes_%d_%d" % (c, g))
+            nc.sync.dma_start(out=tl[:], in_=xb[g][:, :, c * CL:(c + 1) * CL])
+            xbytes[(c, g)] = tl
+
+        wraw = []
+        for r in range(6):
+            wraw.append(keep.tile([P, 1024], BF16, name="wraw%d" % r, tag="wraw%d" % r))
+        wg_rows = w_g.rearrange("(r p) k -> r p k", p=P)
+
+        load_x(0, 0)
+        load_x(0, 1)
+        nc.sync.dma_start(out=wraw[0][:], in_=w_theta)
+        nc.sync.dma_start(out=wraw[1][:], in_=w_phi)
+        load_x(1, 0)
+        nc.sync.dma_start(out=wraw[2][:], in_=wg_rows[0])
+        nc.sync.dma_start(out=wraw[3][:], in_=wg_rows[1])
+        load_x(1, 1)
+        nc.sync.dma_start(out=wraw[4][:], in_=wg_rows[2])
+        nc.sync.dma_start(out=wraw[5][:], in_=wg_rows[3])
+        bth = keep.tile([P, 1], BF16, name="bth", tag="bth")
+        nc.sync.dma_start(out=bth[:], in_=b_theta.rearrange("(p o) -> p o", o=1))
+        bphi = keep.tile([P, 128], BF16, name="bphi", tag="bphi")
+        nc.sync.dma_start(out=bphi[:], in_=b_phi.partition_broadcast(P))
+        bg = keep.tile([P, 512], BF16, name="bg", tag="bg")
+        nc.sync.dma_start(out=bg[:], in_=b_g.partition_broadcast(P))
+        for c in range(2, NCHUNK):
+            for g in range(NPASS):
+                load_x(c, g)
+
+
+        warm = keep.tile([P, 1], F32, name="warm", tag="warm")
+        nc.vector.memset(warm[:], 0.0)
+        warm2 = keep.tile([P, 1], F32, name="warm2", tag="warm2")
+        nc.scalar.activation(out=warm2[:], in_=warm[:], func=ACT.Tanh)
+
+        ident = keep.tile([P, P], F32, name="ident", tag="ident")
+        make_identity(nc, ident[:])
+
+        wide = {}
+        grp = {}
+        xc = {}
+        xs = {}
+
+        def widen(c, g):
+            wd = work.tile([P, 4, CL], BF16, name="wide_%d_%d" % (c, g), tag="wide", bufs=4)
+            wide[(c, g)] = wd
+            src = xbytes[(c, g)]
+            for t in range(4):
+                col = xsc[:, 4 * g + t:4 * g + t + 1]
+                if (c, g) in V_WIDEN:
+                    nc.vector.tensor_scalar(
+                        out=wd[:, t, :], in0=src[:, t, :].bitcast(FP8), scalar1=col, scalar2=None, op0=ALU.mult
+                    )
+                else:
+                    nc.scalar.activation(out=wd[:, t, :], in_=src[:, t, :].bitcast(FP8), func=ACT.Copy, scale=col)
+
+        def inter(c, g):
+            gr = work.tile([P, CL, 4], BF16, name="grp_%d_%d" % (c, g), tag="grp", bufs=3, align_bytes=64)
+            grp[(c, g)] = gr
+            src = wide[(c, g)][:].rearrange("p t (a di j dj) -> p di dj a j t", a=16, di=2, j=8, dj=2)
+            dst = gr[:].rearrange("p (di dj a j) t -> p di dj a j t", di=2, dj=2, a=16, j=8)
+            for di in range(2):
+                nc.vector.tensor_copy(out=dst[:, di], in_=src[:, di])
+
+        def quant(c, g):
+            cd = keep.tile([P, CL], U32, name="xc_%d_%d" % (c, g), tag="xc_%d_%d" % (c, g), align_bytes=64)
+            sc = keep.tile([P, CL], U8, name="xs_%d_%d" % (c, g), tag="xs_%d_%d" % (c, g), align_bytes=64)
+            xc[(c, g)] = cd
+            xs[(c, g)] = sc
+            nc.vector.quantize_mx(
+                out=cd[:].bitcast(FP8X4), scales=sc[:], in_=grp[(c, g)][:].rearrange("p n t -> p (n t)")
+            )
+
+        wgrp = []
+        wc = []
+        wsc = []
+        for g in range(NPASS):
+            wgrp.append(keep.tile([P, 768, 4], BF16, name="wgrp%d" % g, tag="wgrp%d" % g, align_bytes=64))
+            wc.append(keep.tile([P, 768], U32, name="wc%d" % g, tag="wc%d" % g, align_bytes=64))
+            wsc.append(keep.tile([P, 768], U8, name="wsc%d" % g, tag="wsc%d" % g, align_bytes=64))
+
+        def wprep(q, g):
+            bank = psum.tile([P, 2, 2, P], F32, name="wt_%d_%d" % (q, g), tag="G", bufs=5)
+            for r in range(2):
+                words = wraw[2 * q + r][:].bitcast(F32)
+                for u in range(2):
+                    nc.tensor.transpose(bank[:, r, u, :], words[:, 256 * g + u:256 * (g + 1):2], ident[:])
+            dst = wgrp[g][:].rearrange("p o t -> p (o t)").bitcast(F32)[:, 512 * q:512 * (q + 1)]
+            dst = dst.rearrange("p (r o u) -> p r o u", r=2, o=P, u=2)
+            src = bank[:].rearrange("p r u o -> p r o u")
+            if W_COPY_ON_SCALAR[2 * q + g]:
+                nc.scalar.copy(out=dst, in_=src)
+            else:
+                nc.vector.tensor_copy(out=dst, in_=src)
+
+        def wquant(g, lo, hi):
+            flat = wgrp[g][:].rearrange("p o t -> p (o t)")
+            nc.vector.quantize_mx(
+                out=wc[g][:, lo:hi].bitcast(FP8X4), scales=wsc[g][:, lo:hi], in_=flat[:, 4 * lo:4 * hi]
+            )
+
+        tbank = {}
+        fbank = {}
+        gbank = {}
+
+        def mm_theta(c):
+            tb = psum.tile([P, CL], F32, name="T_%d" % c, tag="T", bufs=1)
+            tbank[c] = tb
+            for g in range(NPASS):
+                nc.tensor.matmul_mx(
+                    out=tb[:],
+                    lhsT=wc[g][:, 0:128].bitcast(FP8X4), lhsT_scale=wsc[g][:, 0:128],
+                    rhs=xc[(c, g)][:].bitcast(FP8X4), rhs_scale=xs[(c, g)][:],
+                    start=(g == 0), stop=(g == NPASS - 1),
+                )
+
+        def mm_tile(c, w):
+            if w == 0:
+                fbank[c] = psum.tile([P, 4, P], F32, name="F_%d" % c, tag="F", bufs=1)
+            gb = psum.tile([P, 512], F32, name="G_%d_%d" % (c, w), tag="G", bufs=5)
+            gbank[(c, w)] = gb
+            cols = slice(P * w, P * (w + 1))
+            for g in range(NPASS):
+                lhsT = xc[(c, g)][:, cols].bitcast(FP8X4)
+                lsc = xs[(c, g)][:, cols]
+                nc.tensor.matmul_mx(
+                    out=gb[:], lhsT=lhsT, lhsT_scale=lsc,
+                    rhs=wc[g][:, 256:768].bitcast(FP8X4), rhs_scale=wsc[g][:, 256:768],
+                    start=(g == 0), stop=(g == NPASS - 1),
+                )
+                nc.tensor.matmul_mx(
+                    out=fbank[c][:, w, :], lhsT=lhsT, lhsT_scale=lsc,
+                    rhs=wc[g][:, 128:256].bitcast(FP8X4), rhs_scale=wsc[g][:, 128:256],
+                    start=(g == 0), stop=(g == NPASS - 1),
+                )
+
+        acc = {}
+
+        def g_first(c):
+            acc[c] = work.tile([P, 512], F32, name="acc_%d" % c, tag="acc", bufs=2)
+            nc.scalar.copy(out=acc[c][:], in_=gbank[(c, 0)][:])
+
+        def g_max(c, w):
+            nc.vector.tensor_tensor(out=acc[c][:], in0=gbank[(c, w)][:], in1=acc[c][:], op=ALU.max)
+
+        def g_last(c):
+            go = work.tile([P, 512], F32, name="gout_%d" % c, tag="gout", bufs=2)
+            nc.vector.tensor_tensor(out=go[:], in0=acc[c][:], in1=bg[:], op=ALU.add)
+            nc.sync.dma_start(out=out_2[0, P * c:P * (c + 1), :], in_=go[:])
+
+        def phi_all(c):
+            pr = work.tile([P, P], F32, name="pr_%d" % c, tag="pr", bufs=2)
+            nc.vector.tensor_reduce(out=pr[:], in_=fbank[c][:].rearrange("p w k -> p k w"), axis=AX.X, op=ALU.max)
+            pb = work.tile([P, P], F32, name="pb_%d" % c, tag="pb", bufs=2)
+            nc.vector.tensor_tensor(out=pb[:], in0=pr[:], in1=bphi[:], op=ALU.add)
+            po = work.tile([P, P], F32, name="po_%d" % c, tag="po", bufs=2)
+            nc.scalar.activation(out=po[:], in_=pb[:], func=ACT.Tanh)
+            nc.sync.dma_start(out=out_1[0, P * c:P * (c + 1), :], in_=po[:])
+
+        th = {}
+
+        def theta_tanh(c):
+            th[c] = work.tile([P, CL], F32, name="th_%d" % c, tag="th", bufs=2)
+            src = tbank[c][:].rearrange("p (di dj a j) -> p dj a di j", di=2, dj=2, a=16, j=8)
+            dst = th[c][:].rearrange("p (dj a di j) -> p dj a di j", dj=2, a=16, di=2, j=8)
+            for dj in range(2):
+                nc.scalar.activation(out=dst[:, dj], in_=src[:, dj], func=ACT.Tanh, bias=bth[:, 0:1])
+
+        out0v = out_0[0].rearrange("(c f p dj) k -> c p f (dj k)", c=NCHUNK, f=2, p=P, dj=2)
+
+        def theta_out(c):
+            ub = psum.tile([P, 4, P], F32, name="U_%d" % c, tag="U", bufs=1)
+            for dj in range(2):
+                for f in range(2):
+                    b = 2 * dj + f
+                    nc.tensor.transpose(ub[:, 2 * f + dj, :], th[c][:, P * b:P * (b + 1)], ident[:])
+            to = work.tile([P, 4, P], F32, name="tho_%d" % c, tag="tho", bufs=2)
+            if U_COPY_ON_SCALAR:
+                nc.scalar.copy(out=to[:], in_=ub[:])
+            else:
+                nc.vector.tensor_copy(out=to[:], in_=ub[:])
+            nc.sync.dma_start(out=out0v[c], in_=to[:].rearrange("p (f dj) k -> p f (dj k)", f=2))
+
+        widen(0, 0)
+        widen(0, 1)
+        inter(0, 0)
+        wprep(0, 0)
+        wprep(0, 1)
+        quant(0, 0)
+        inter(0, 1)
+        wprep(1, 0)
+        wprep(1, 1)
+        quant(0, 1)
+        wprep(2, 0)
+        wprep(2, 1)
+        widen(1, 0)
+        for g in range(NPASS):
+            wquant(g, 0, 256)
+            wquant(g, 256, 768)
+        widen(1, 1)
+
+        for c in range(NCHUNK):
+            nxt = c + 1 < NCHUNK
+            mm_theta(c)
+            for w in range(4):
+                mm_tile(c, w)
+            if nxt:
+                inter(c + 1, 0)
+            if c + 2 < NCHUNK:
+                widen(c + 2, 0)
+            theta_tanh(c)
+            g_first(c)
+            g_max(c, 1)
+            if nxt:
+                quant(c + 1, 0)
+                inter(c + 1, 1)
+            theta_out(c)
+            g_max(c, 2)
+            if nxt:
+                quant(c + 1, 1)
+            g_max(c, 3)
+            if c + 2 < NCHUNK:
+                widen(c + 2, 1)
+            phi_all(c)
+            g_last(c)

@@ -20,9 +20,37 @@ NCHUNK = 4
 NPASS = 2
 CL = 512
 
-V_WIDEN = ((0, 0),)
-W_COPY_ON_SCALAR = (True, True, True, True, True, True)
-U_COPY_ON_SCALAR = True
+V_WIDEN = ((0, 0, 1), (0, 0, 2), (0, 0, 3), (0, 1, 2), (1, 0, 1), (1, 0, 3), (1, 1, 0))
+S_INTER = ((3, 0, 1),)
+G_INTER = {}
+V_WCOPY = ()
+V_UCOPY = ()
+LOADS = ('x00', 'x01', 'w0', 'w1', 'x10', 'w2', 'w3', 'w4', 'w5', 'x11', 'bias', 'x20', 'x21', 'x30', 'x31')
+ORDER = (
+    "widen_0_0_0", "widen_0_0_1", "widen_0_0_2", "widen_0_0_3", "widen_0_1_0", "widen_0_1_2", "inter_0_0_0", "widen_0_1_1",
+    "inter_0_0_1", "widen_0_1_3", "wT_0_0", "wT_0_1", "quant_0_0", "wcopy_0_0", "inter_0_1_0", "wcopy_0_1",
+    "widen_1_0_0", "wq_0_0", "wT_1_0", "wq_1_0", "widen_1_0_2", "inter_0_1_1", "wT_1_1", "wcopy_1_0",
+    "widen_1_0_1", "wT_2_0", "quant_0_1", "wcopy_1_1", "wT_2_1", "widen_1_0_3", "wcopy_2_0", "widen_1_1_0",
+    "mmT_0_0", "inter_1_0_0", "wcopy_2_1", "widen_1_1_1", "wq_0_1", "widen_1_1_2", "wq_1_1", "mmG_0_0_0",
+    "widen_1_1_3", "mmG_0_1_0", "inter_1_0_1", "mmG_0_2_0", "widen_2_0_0", "mmG_0_3_0", "inter_1_1_0", "mmG_0_0_1",
+    "widen_2_0_1", "mmT_0_1", "mmG_0_1_1", "quant_1_0", "gread_0_0", "mmG_0_2_1", "mmG_0_3_1", "inter_1_1_1",
+    "ttanh_0_0", "mmF_0_0", "mmF_0_1", "ttanh_0_1", "mmF_0_2", "mmF_0_3", "gread_0_1", "widen_2_0_2",
+    "tT_0", "mmT_1_0", "quant_1_1", "widen_2_0_3", "mmG_1_0_0", "gread_0_2", "ucopy_0", "mmG_1_1_0",
+    "mmG_1_2_0", "phired_0", "widen_2_1_0", "mmG_1_3_0", "st_t0", "gread_0_3", "mmG_1_0_1", "widen_2_1_1",
+    "mmT_1_1", "inter_2_0_0", "mmG_1_1_1", "widen_2_1_2", "mmG_1_2_1", "mmG_1_3_1", "gread_1_0", "bias_0",
+    "mmF_1_0", "mmF_1_1", "ttanh_1_0", "mmF_1_2", "mmF_1_3", "inter_2_0_1", "ttanh_1_1", "st_g0",
+    "tT_1", "widen_2_1_3", "gread_1_1", "widen_3_0_0", "quant_2_0", "ucopy_1", "gread_1_2", "widen_3_0_1",
+    "mmT_2_0", "st_t1", "phired_1", "mmG_2_0_0", "widen_3_0_2", "mmG_2_1_0", "gread_1_3", "mmG_2_2_0",
+    "widen_3_0_3", "mmG_2_3_0", "inter_2_1_0", "widen_3_1_0", "bias_1", "inter_3_0_1", "inter_2_1_1", "st_g1",
+    "widen_3_1_1", "inter_3_0_0", "widen_3_1_2", "quant_2_1", "widen_3_1_3", "quant_3_0", "mmG_2_0_1", "phit_0",
+    "phit_1", "mmT_2_1", "inter_3_1_0", "st_p0", "mmG_2_1_1", "gread_2_0", "st_p1", "mmG_2_2_1",
+    "inter_3_1_1", "mmG_2_3_1", "ttanh_2_0", "mmF_2_0", "ttanh_2_1", "mmF_2_1", "mmF_2_2", "gread_2_1",
+    "mmF_2_3", "tT_2", "quant_3_1", "mmT_3_0", "ucopy_2", "mmG_3_0_0", "gread_2_2", "mmG_3_1_0",
+    "mmG_3_2_0", "phired_2", "st_t2", "mmG_3_3_0", "gread_2_3", "mmG_3_0_1", "mmT_3_1", "mmG_3_1_1",
+    "gread_3_0", "bias_2", "mmG_3_2_1", "mmG_3_3_1", "ttanh_3_0", "mmF_3_0", "ttanh_3_1", "gread_3_1",
+    "mmF_3_1", "mmF_3_2", "phit_2", "st_g2", "mmF_3_3", "tT_3", "st_p2", "gread_3_2",
+    "ucopy_3", "phired_3", "gread_3_3", "st_t3", "bias_3", "phit_3", "st_g3", "st_p3",
+)
 
 
 def tile_selfattention3d_pb_kernel(
@@ -31,114 +59,130 @@ def tile_selfattention3d_pb_kernel(
     nc = tc.nc
     with ExitStack() as ctx:
         keep = ctx.enter_context(tc.tile_pool(name="keep", bufs=1))
-        work = ctx.enter_context(tc.tile_pool(name="work", bufs=2))
         psum = ctx.enter_context(tc.psum_pool(name="psum", bufs=1))
+        ctx.enter_context(tc.manual_schedule())
 
-        xsc = keep.tile([P, 8], F32, name="xsc", tag="xsc")
-        nc.sync.dma_start(
+        def sb(shape, dtype, name, align=None):
+            if align is None:
+                return keep.tile(shape, dtype, name=name, tag=name)
+            return keep.tile(shape, dtype, name=name, tag=name, align_bytes=align)
+
+        xsc = sb([P, 8], F32, "xsc")
+        xb = x_bytes[0].rearrange("(g p t) f i j -> g p t (f i j)", g=NPASS, p=P, t=4)
+        wg_rows = w_g.rearrange("(r p) k -> r p k", p=P)
+        xbytes = {}
+        wraw = {}
+        bth = sb([P, 1], BF16, "bth")
+        bgp = sb([P, 640], BF16, "bgp")
+
+        nc.scalar.dma_start(
             out=xsc[:].rearrange("p (g t) -> p g t", g=NPASS),
             in_=x_scale.rearrange("o k a b c -> (o k a b c)").rearrange("(g p t) -> p g t", g=NPASS, p=P, t=4),
         )
-        xb = x_bytes[0].rearrange("(g p t) f i j -> g p t (f i j)", g=NPASS, p=P, t=4)
-        xbytes = {}
+        for nm in LOADS:
+            if nm[0] == "x":
+                c = int(nm[1])
+                g = int(nm[2])
+                tl = sb([P, 4, CL], U8, "xbytes_%d_%d" % (c, g))
+                nc.sync.dma_start(out=tl[:], in_=xb[g][:, :, c * CL:(c + 1) * CL])
+                xbytes[(c, g)] = tl
+            elif nm[0] == "w":
+                r = int(nm[1])
+                tl = sb([P, 1024], BF16, "wraw%d" % r)
+                wraw[r] = tl
+                if r == 0:
+                    nc.sync.dma_start(out=tl[:], in_=w_theta)
+                elif r == 1:
+                    nc.sync.dma_start(out=tl[:], in_=w_phi)
+                else:
+                    nc.sync.dma_start(out=tl[:], in_=wg_rows[r - 2])
+            else:
+                nc.sync.dma_start(out=bth[:], in_=b_theta.rearrange("(p o) -> p o", o=1))
+                nc.sync.dma_start(out=bgp[:, 0:512], in_=b_g.partition_broadcast(P))
+                nc.sync.dma_start(out=bgp[:, 512:640], in_=b_phi.partition_broadcast(P))
 
-        def load_x(c, g):
-            tl = keep.tile([P, 4, CL], U8, name="xbytes_%d_%d" % (c, g), tag="xbytes_%d_%d" % (c, g))
-            nc.sync.dma_start(out=tl[:], in_=xb[g][:, :, c * CL:(c + 1) * CL])
-            xbytes[(c, g)] = tl
-
-        wraw = []
-        for r in range(6):
-            wraw.append(keep.tile([P, 1024], BF16, name="wraw%d" % r, tag="wraw%d" % r))
-        wg_rows = w_g.rearrange("(r p) k -> r p k", p=P)
-
-        load_x(0, 0)
-        load_x(0, 1)
-        nc.sync.dma_start(out=wraw[0][:], in_=w_theta)
-        nc.sync.dma_start(out=wraw[1][:], in_=w_phi)
-        load_x(1, 0)
-        nc.sync.dma_start(out=wraw[2][:], in_=wg_rows[0])
-        nc.sync.dma_start(out=wraw[3][:], in_=wg_rows[1])
-        load_x(1, 1)
-        nc.sync.dma_start(out=wraw[4][:], in_=wg_rows[2])
-        nc.sync.dma_start(out=wraw[5][:], in_=wg_rows[3])
-        bth = keep.tile([P, 1], BF16, name="bth", tag="bth")
-        nc.sync.dma_start(out=bth[:], in_=b_theta.rearrange("(p o) -> p o", o=1))
-        bphi = keep.tile([P, 128], BF16, name="bphi", tag="bphi")
-        nc.sync.dma_start(out=bphi[:], in_=b_phi.partition_broadcast(P))
-        bg = keep.tile([P, 512], BF16, name="bg", tag="bg")
-        nc.sync.dma_start(out=bg[:], in_=b_g.partition_broadcast(P))
-        for c in range(2, NCHUNK):
-            for g in range(NPASS):
-                load_x(c, g)
-
-
-        warm = keep.tile([P, 1], F32, name="warm", tag="warm")
+        warm = sb([P, 1], F32, "warm")
         nc.vector.memset(warm[:], 0.0)
-        warm2 = keep.tile([P, 1], F32, name="warm2", tag="warm2")
+        warm2 = sb([P, 1], F32, "warm2")
         nc.scalar.activation(out=warm2[:], in_=warm[:], func=ACT.Tanh)
 
-        ident = keep.tile([P, P], F32, name="ident", tag="ident")
+        ident = sb([P, P], F32, "ident")
         make_identity(nc, ident[:])
 
         wide = {}
         grp = {}
         xc = {}
         xs = {}
+        flags = {}
+        for c in range(NCHUNK):
+            for g in range(NPASS):
+                wide[(c, g)] = sb([P, 4, CL], BF16, "wide_%d_%d" % (c, g))
+                grp[(c, g)] = sb([P, CL, 4], BF16, "grp_%d_%d" % (c, g), 64)
+                xc[(c, g)] = sb([P, CL], U32, "xc_%d_%d" % (c, g), 64)
+                xs[(c, g)] = sb([P, CL], U8, "xs_%d_%d" % (c, g), 64)
 
-        def widen(c, g):
-            wd = work.tile([P, 4, CL], BF16, name="wide_%d_%d" % (c, g), tag="wide", bufs=4)
-            wide[(c, g)] = wd
-            src = xbytes[(c, g)]
-            for t in range(4):
-                col = xsc[:, 4 * g + t:4 * g + t + 1]
-                if (c, g) in V_WIDEN:
-                    nc.vector.tensor_scalar(
-                        out=wd[:, t, :], in0=src[:, t, :].bitcast(FP8), scalar1=col, scalar2=None, op0=ALU.mult
-                    )
-                else:
-                    nc.scalar.activation(out=wd[:, t, :], in_=src[:, t, :].bitcast(FP8), func=ACT.Copy, scale=col)
+        def widen(c, g, t):
+            col = xsc[:, 4 * g + t:4 * g + t + 1]
+            dst = wide[(c, g)][:, t, :]
+            src = xbytes[(c, g)][:, t, :].bitcast(FP8)
+            if (c, g, t) in V_WIDEN:
+                nc.vector.tensor_scalar(out=dst, in0=src, scalar1=col, scalar2=None, op0=ALU.mult)
+            else:
+                nc.scalar.activation(out=dst, in_=src, func=ACT.Copy, scale=col)
 
-        def inter(c, g):
-            gr = work.tile([P, CL, 4], BF16, name="grp_%d_%d" % (c, g), tag="grp", bufs=3, align_bytes=64)
-            grp[(c, g)] = gr
+        def flag(c):
+            flags[c] = sb([P, 1], F32, "flag_%d" % c)
+            nc.vector.memset(flags[c][:], 1.0)
+
+        def inter(c, g, di):
             src = wide[(c, g)][:].rearrange("p t (a di j dj) -> p di dj a j t", a=16, di=2, j=8, dj=2)
-            dst = gr[:].rearrange("p (di dj a j) t -> p di dj a j t", di=2, dj=2, a=16, j=8)
-            for di in range(2):
+            dst = grp[(c, g)][:].rearrange("p (di dj a j) t -> p di dj a j t", di=2, dj=2, a=16, j=8)
+            if (c, g, di) in S_INTER:
+                for dj in range(2):
+                    nc.scalar.copy(out=dst[:, di, dj], in_=src[:, di, dj])
+            elif (c, g, di) in G_INTER:
+                one = flags[G_INTER[(c, g, di)]]
+                for dj in range(2):
+                    nc.gpsimd.tensor_scalar(
+                        out=dst[:, di, dj], in0=src[:, di, dj], scalar1=one[:, 0:1], scalar2=0.0,
+                        op0=ALU.mult, op1=ALU.add,
+                    )
+            else:
                 nc.vector.tensor_copy(out=dst[:, di], in_=src[:, di])
 
         def quant(c, g):
-            cd = keep.tile([P, CL], U32, name="xc_%d_%d" % (c, g), tag="xc_%d_%d" % (c, g), align_bytes=64)
-            sc = keep.tile([P, CL], U8, name="xs_%d_%d" % (c, g), tag="xs_%d_%d" % (c, g), align_bytes=64)
-            xc[(c, g)] = cd
-            xs[(c, g)] = sc
             nc.vector.quantize_mx(
-                out=cd[:].bitcast(FP8X4), scales=sc[:], in_=grp[(c, g)][:].rearrange("p n t -> p (n t)")
+                out=xc[(c, g)][:].bitcast(FP8X4), scales=xs[(c, g)][:], in_=grp[(c, g)][:].rearrange("p n t -> p (n t)")
             )
 
         wgrp = []
         wc = []
         wsc = []
         for g in range(NPASS):
-            wgrp.append(keep.tile([P, 768, 4], BF16, name="wgrp%d" % g, tag="wgrp%d" % g, align_bytes=64))
-            wc.append(keep.tile([P, 768], U32, name="wc%d" % g, tag="wc%d" % g, align_bytes=64))
-            wsc.append(keep.tile([P, 768], U8, name="wsc%d" % g, tag="wsc%d" % g, align_bytes=64))
+            wgrp.append(sb([P, 768, 4], BF16, "wgrp%d" % g, 64))
+            wc.append(sb([P, 768], U32, "wc%d" % g, 64))
+            wsc.append(sb([P, 768], U8, "wsc%d" % g, 64))
+        wbank = {}
 
-        def wprep(q, g):
+        def wT(q, g):
             bank = psum.tile([P, 2, 2, P], F32, name="wt_%d_%d" % (q, g), tag="G", bufs=5)
+            wbank[(q, g)] = bank
             for r in range(2):
                 words = wraw[2 * q + r][:].bitcast(F32)
                 for u in range(2):
                     nc.tensor.transpose(bank[:, r, u, :], words[:, 256 * g + u:256 * (g + 1):2], ident[:])
+
+        def wcopy(q, g):
             dst = wgrp[g][:].rearrange("p o t -> p (o t)").bitcast(F32)[:, 512 * q:512 * (q + 1)]
             dst = dst.rearrange("p (r o u) -> p r o u", r=2, o=P, u=2)
-            src = bank[:].rearrange("p r u o -> p r o u")
-            if W_COPY_ON_SCALAR[2 * q + g]:
-                nc.scalar.copy(out=dst, in_=src)
-            else:
+            src = wbank[(q, g)][:].rearrange("p r u o -> p r o u")
+            if (q, g) in V_WCOPY:
                 nc.vector.tensor_copy(out=dst, in_=src)
+            else:
+                nc.scalar.copy(out=dst, in_=src)
 
-        def wquant(g, lo, hi):
+        def wq(g, part):
+            lo, hi = ((0, 256), (256, 768))[part]
             flat = wgrp[g][:].rearrange("p o t -> p (o t)")
             nc.vector.quantize_mx(
                 out=wc[g][:, lo:hi].bitcast(FP8X4), scales=wsc[g][:, lo:hi], in_=flat[:, 4 * lo:4 * hi]
@@ -148,123 +192,105 @@ def tile_selfattention3d_pb_kernel(
         fbank = {}
         gbank = {}
 
-        def mm_theta(c):
-            tb = psum.tile([P, CL], F32, name="T_%d" % c, tag="T", bufs=1)
-            tbank[c] = tb
-            for g in range(NPASS):
-                nc.tensor.matmul_mx(
-                    out=tb[:],
-                    lhsT=wc[g][:, 0:128].bitcast(FP8X4), lhsT_scale=wsc[g][:, 0:128],
-                    rhs=xc[(c, g)][:].bitcast(FP8X4), rhs_scale=xs[(c, g)][:],
-                    start=(g == 0), stop=(g == NPASS - 1),
-                )
+        def mmT(c, g):
+            if g == 0:
+                tbank[c] = psum.tile([P, CL], F32, name="T_%d" % c, tag="T", bufs=1)
+            nc.tensor.matmul_mx(
+                out=tbank[c][:],
+                lhsT=wc[g][:, 0:128].bitcast(FP8X4), lhsT_scale=wsc[g][:, 0:128],
+                rhs=xc[(c, g)][:].bitcast(FP8X4), rhs_scale=xs[(c, g)][:],
+                start=(g == 0), stop=(g == NPASS - 1),
+            )
 
-        def mm_tile(c, w):
+        def mmG(c, w, g):
+            if g == 0:
+                gbank[(c, w)] = psum.tile([P, 512], F32, name="G_%d_%d" % (c, w), tag="G", bufs=5)
+            cols = slice(P * w, P * (w + 1))
+            nc.tensor.matmul_mx(
+                out=gbank[(c, w)][:],
+                lhsT=xc[(c, g)][:, cols].bitcast(FP8X4), lhsT_scale=xs[(c, g)][:, cols],
+                rhs=wc[g][:, 256:768].bitcast(FP8X4), rhs_scale=wsc[g][:, 256:768],
+                start=(g == 0), stop=(g == NPASS - 1),
+            )
+
+        def mmF(c, w):
             if w == 0:
                 fbank[c] = psum.tile([P, 4, P], F32, name="F_%d" % c, tag="F", bufs=1)
-            gb = psum.tile([P, 512], F32, name="G_%d_%d" % (c, w), tag="G", bufs=5)
-            gbank[(c, w)] = gb
             cols = slice(P * w, P * (w + 1))
             for g in range(NPASS):
-                lhsT = xc[(c, g)][:, cols].bitcast(FP8X4)
-                lsc = xs[(c, g)][:, cols]
                 nc.tensor.matmul_mx(
-                    out=gb[:], lhsT=lhsT, lhsT_scale=lsc,
-                    rhs=wc[g][:, 256:768].bitcast(FP8X4), rhs_scale=wsc[g][:, 256:768],
-                    start=(g == 0), stop=(g == NPASS - 1),
-                )
-                nc.tensor.matmul_mx(
-                    out=fbank[c][:, w, :], lhsT=lhsT, lhsT_scale=lsc,
+                    out=fbank[c][:, w, :],
+                    lhsT=xc[(c, g)][:, cols].bitcast(FP8X4), lhsT_scale=xs[(c, g)][:, cols],
                     rhs=wc[g][:, 128:256].bitcast(FP8X4), rhs_scale=wsc[g][:, 128:256],
                     start=(g == 0), stop=(g == NPASS - 1),
                 )
 
         acc = {}
-
-        def g_first(c):
-            acc[c] = work.tile([P, 512], F32, name="acc_%d" % c, tag="acc", bufs=2)
-            nc.scalar.copy(out=acc[c][:], in_=gbank[(c, 0)][:])
-
-        def g_max(c, w):
-            nc.vector.tensor_tensor(out=acc[c][:], in0=gbank[(c, w)][:], in1=acc[c][:], op=ALU.max)
-
-        def g_last(c):
-            go = work.tile([P, 512], F32, name="gout_%d" % c, tag="gout", bufs=2)
-            nc.vector.tensor_tensor(out=go[:], in0=acc[c][:], in1=bg[:], op=ALU.add)
-            nc.sync.dma_start(out=out_2[0, P * c:P * (c + 1), :], in_=go[:])
-
-        def phi_all(c):
-            pr = work.tile([P, P], F32, name="pr_%d" % c, tag="pr", bufs=2)
-            nc.vector.tensor_reduce(out=pr[:], in_=fbank[c][:].rearrange("p w k -> p k w"), axis=AX.X, op=ALU.max)
-            pb = work.tile([P, P], F32, name="pb_%d" % c, tag="pb", bufs=2)
-            nc.vector.tensor_tensor(out=pb[:], in0=pr[:], in1=bphi[:], op=ALU.add)
-            po = work.tile([P, P], F32, name="po_%d" % c, tag="po", bufs=2)
-            nc.scalar.activation(out=po[:], in_=pb[:], func=ACT.Tanh)
-            nc.sync.dma_start(out=out_1[0, P * c:P * (c + 1), :], in_=po[:])
-
+        gp = {}
+        po = {}
         th = {}
+        tho = {}
+        ubank = {}
+        for c in range(NCHUNK):
+            acc[c] = sb([P, 640], F32, "acc_%d" % c)
+            gp[c] = sb([P, 640], F32, "gp_%d" % c)
+            po[c] = sb([P, P], F32, "po_%d" % c)
+            th[c] = sb([P, CL], F32, "th_%d" % c)
+            tho[c] = sb([P, 4, P], F32, "tho_%d" % c)
 
-        def theta_tanh(c):
-            th[c] = work.tile([P, CL], F32, name="th_%d" % c, tag="th", bufs=2)
+        def gread(c, w):
+            if w == 0:
+                nc.scalar.copy(out=acc[c][:, 0:512], in_=gbank[(c, 0)][:])
+            else:
+                nc.vector.tensor_tensor(out=acc[c][:, 0:512], in0=gbank[(c, w)][:], in1=acc[c][:, 0:512], op=ALU.max)
+
+        def phired(c):
+            nc.vector.tensor_reduce(
+                out=acc[c][:, 512:640], in_=fbank[c][:].rearrange("p w k -> p k w"), axis=AX.X, op=ALU.max
+            )
+
+        def bias(c):
+            nc.vector.tensor_tensor(out=gp[c][:], in0=acc[c][:], in1=bgp[:], op=ALU.add)
+
+        def phit(c):
+            nc.scalar.activation(out=po[c][:], in_=gp[c][:, 512:640], func=ACT.Tanh)
+
+        def ttanh(c, dj):
             src = tbank[c][:].rearrange("p (di dj a j) -> p dj a di j", di=2, dj=2, a=16, j=8)
             dst = th[c][:].rearrange("p (dj a di j) -> p dj a di j", dj=2, a=16, di=2, j=8)
-            for dj in range(2):
-                nc.scalar.activation(out=dst[:, dj], in_=src[:, dj], func=ACT.Tanh, bias=bth[:, 0:1])
+            nc.scalar.activation(out=dst[:, dj], in_=src[:, dj], func=ACT.Tanh, bias=bth[:, 0:1])
 
-        out0v = out_0[0].rearrange("(c f p dj) k -> c p f (dj k)", c=NCHUNK, f=2, p=P, dj=2)
-
-        def theta_out(c):
-            ub = psum.tile([P, 4, P], F32, name="U_%d" % c, tag="U", bufs=1)
+        def tT(c):
+            ubank[c] = psum.tile([P, 4, P], F32, name="U_%d" % c, tag="U", bufs=1)
             for dj in range(2):
                 for f in range(2):
                     b = 2 * dj + f
-                    nc.tensor.transpose(ub[:, 2 * f + dj, :], th[c][:, P * b:P * (b + 1)], ident[:])
-            to = work.tile([P, 4, P], F32, name="tho_%d" % c, tag="tho", bufs=2)
-            if U_COPY_ON_SCALAR:
-                nc.scalar.copy(out=to[:], in_=ub[:])
+                    nc.tensor.transpose(ubank[c][:, 2 * f + dj, :], th[c][:, P * b:P * (b + 1)], ident[:])
+
+        def ucopy(c):
+            if c in V_UCOPY:
+                nc.vector.tensor_copy(out=tho[c][:], in_=ubank[c][:])
             else:
-                nc.vector.tensor_copy(out=to[:], in_=ub[:])
-            nc.sync.dma_start(out=out0v[c], in_=to[:].rearrange("p (f dj) k -> p f (dj k)", f=2))
+                nc.scalar.copy(out=tho[c][:], in_=ubank[c][:])
 
-        widen(0, 0)
-        widen(0, 1)
-        inter(0, 0)
-        wprep(0, 0)
-        wprep(0, 1)
-        quant(0, 0)
-        inter(0, 1)
-        wprep(1, 0)
-        wprep(1, 1)
-        quant(0, 1)
-        wprep(2, 0)
-        wprep(2, 1)
-        widen(1, 0)
-        for g in range(NPASS):
-            wquant(g, 0, 256)
-            wquant(g, 256, 768)
-        widen(1, 1)
+        out0v = out_0[0].rearrange("(c f p dj) k -> c p f (dj k)", c=NCHUNK, f=2, p=P, dj=2)
 
-        for c in range(NCHUNK):
-            nxt = c + 1 < NCHUNK
-            mm_theta(c)
-            for w in range(4):
-                mm_tile(c, w)
-            if nxt:
-                inter(c + 1, 0)
-            if c + 2 < NCHUNK:
-                widen(c + 2, 0)
-            theta_tanh(c)
-            g_first(c)
-            g_max(c, 1)
-            if nxt:
-                quant(c + 1, 0)
-                inter(c + 1, 1)
-            theta_out(c)
-            g_max(c, 2)
-            if nxt:
-                quant(c + 1, 1)
-            g_max(c, 3)
-            if c + 2 < NCHUNK:
-                widen(c + 2, 1)
-            phi_all(c)
-            g_last(c)
+        def st(kind, c):
+            if kind == "g":
+                nc.sync.dma_start(out=out_2[0, P * c:P * (c + 1), :], in_=gp[c][:, 0:512])
+            elif kind == "p":
+                nc.sync.dma_start(out=out_1[0, P * c:P * (c + 1), :], in_=po[c][:])
+            else:
+                nc.sync.dma_start(out=out0v[c], in_=tho[c][:].rearrange("p (f dj) k -> p f (dj k)", f=2))
+
+        fns = {
+            "widen": widen, "flag": flag, "inter": inter, "quant": quant, "wT": wT, "wcopy": wcopy, "wq": wq,
+            "mmT": mmT, "mmG": mmG, "mmF": mmF, "gread": gread, "phired": phired, "bias": bias, "phit": phit,
+            "ttanh": ttanh, "tT": tT, "ucopy": ucopy,
+        }
+        for item in ORDER:
+            parts = item.split("_")
+            if parts[0] == "st":
+                st(parts[1][0], int(parts[1][1]))
+            else:
+                fns[parts[0]](*[int(v) for v in parts[1:]])

@@ -25,31 +25,33 @@ S_INTER = ((3, 0, 1),)
 G_INTER = {}
 V_WCOPY = ()
 V_UCOPY = ()
-LOADS = ('x00', 'x01', 'w0', 'w1', 'x10', 'w2', 'w3', 'w4', 'w5', 'x11', 'bias', 'x20', 'x21', 'x30', 'x31')
+V_BCOPY = False
+LOADS = ('x00', 'x01', 'bias', 'w0', 'w1', 'x10', 'w2', 'w3', 'w4', 'w5', 'x11', 'x20', 'x21', 'x30', 'x31')
 ORDER = (
     "widen_0_0_0", "widen_0_0_1", "widen_0_0_2", "widen_0_0_3", "widen_0_1_0", "widen_0_1_2", "inter_0_0_0", "widen_0_1_1",
-    "inter_0_0_1", "widen_0_1_3", "wT_0_0", "wT_0_1", "quant_0_0", "wcopy_0_0", "inter_0_1_0", "wcopy_0_1",
-    "widen_1_0_0", "wq_0_0", "wT_1_0", "wq_1_0", "widen_1_0_2", "inter_0_1_1", "wT_1_1", "wcopy_1_0",
-    "widen_1_0_1", "wT_2_0", "quant_0_1", "wcopy_1_1", "wT_2_1", "widen_1_0_3", "wcopy_2_0", "widen_1_1_0",
-    "mmT_0_0", "inter_1_0_0", "wcopy_2_1", "widen_1_1_1", "wq_0_1", "widen_1_1_2", "wq_1_1", "mmG_0_0_0",
-    "widen_1_1_3", "mmG_0_1_0", "inter_1_0_1", "mmG_0_2_0", "widen_2_0_0", "mmG_0_3_0", "inter_1_1_0", "mmG_0_0_1",
-    "widen_2_0_1", "mmT_0_1", "mmG_0_1_1", "quant_1_0", "gread_0_0", "mmG_0_2_1", "mmG_0_3_1", "inter_1_1_1",
-    "ttanh_0_0", "mmF_0_0", "mmF_0_1", "ttanh_0_1", "mmF_0_2", "mmF_0_3", "gread_0_1", "widen_2_0_2",
-    "tT_0", "mmT_1_0", "quant_1_1", "widen_2_0_3", "mmG_1_0_0", "gread_0_2", "ucopy_0", "mmG_1_1_0",
-    "mmG_1_2_0", "phired_0", "widen_2_1_0", "mmG_1_3_0", "st_t0", "gread_0_3", "mmG_1_0_1", "widen_2_1_1",
-    "mmT_1_1", "inter_2_0_0", "mmG_1_1_1", "widen_2_1_2", "mmG_1_2_1", "mmG_1_3_1", "gread_1_0", "bias_0",
-    "mmF_1_0", "mmF_1_1", "ttanh_1_0", "mmF_1_2", "mmF_1_3", "inter_2_0_1", "ttanh_1_1", "st_g0",
-    "tT_1", "widen_2_1_3", "gread_1_1", "widen_3_0_0", "quant_2_0", "ucopy_1", "gread_1_2", "widen_3_0_1",
-    "mmT_2_0", "st_t1", "phired_1", "mmG_2_0_0", "widen_3_0_2", "mmG_2_1_0", "gread_1_3", "mmG_2_2_0",
-    "widen_3_0_3", "mmG_2_3_0", "inter_2_1_0", "widen_3_1_0", "bias_1", "inter_3_0_1", "inter_2_1_1", "st_g1",
-    "widen_3_1_1", "inter_3_0_0", "widen_3_1_2", "quant_2_1", "widen_3_1_3", "quant_3_0", "mmG_2_0_1", "phit_0",
-    "phit_1", "mmT_2_1", "inter_3_1_0", "st_p0", "mmG_2_1_1", "gread_2_0", "st_p1", "mmG_2_2_1",
-    "inter_3_1_1", "mmG_2_3_1", "ttanh_2_0", "mmF_2_0", "ttanh_2_1", "mmF_2_1", "mmF_2_2", "gread_2_1",
-    "mmF_2_3", "tT_2", "quant_3_1", "mmT_3_0", "ucopy_2", "mmG_3_0_0", "gread_2_2", "mmG_3_1_0",
-    "mmG_3_2_0", "phired_2", "st_t2", "mmG_3_3_0", "gread_2_3", "mmG_3_0_1", "mmT_3_1", "mmG_3_1_1",
-    "gread_3_0", "bias_2", "mmG_3_2_1", "mmG_3_3_1", "ttanh_3_0", "mmF_3_0", "ttanh_3_1", "gread_3_1",
-    "mmF_3_1", "mmF_3_2", "phit_2", "st_g2", "mmF_3_3", "tT_3", "st_p2", "gread_3_2",
-    "ucopy_3", "phired_3", "gread_3_3", "st_t3", "bias_3", "phit_3", "st_g3", "st_p3",
+    "inter_0_0_1", "widen_0_1_3", "wT_0_0", "wT_0_1", "quant_0_0", "wcopy_0_0", "bmm", "inter_0_1_0",
+    "wcopy_0_1", "wq_0_0", "bcopy", "wT_1_0", "inter_0_1_1", "widen_1_0_0", "wT_1_1", "wq_1_0",
+    "wcopy_1_0", "quant_0_1", "wT_2_0", "wcopy_1_1", "widen_1_0_1", "wT_2_1", "widen_1_0_3", "widen_1_0_2",
+    "widen_1_1_0", "mmT_0_0", "wcopy_2_0", "inter_1_0_0", "wcopy_2_1", "wq_0_1", "widen_1_1_1", "wq_1_1",
+    "widen_1_1_2", "mmG_0_0_0", "mmG_0_1_0", "inter_1_0_1", "widen_1_1_3", "mmG_0_2_0", "mmG_0_3_0", "widen_2_0_0",
+    "mmG_0_0_1", "inter_1_1_0", "mmT_0_1", "widen_2_0_1", "mmG_0_1_1", "quant_1_0", "mmG_0_2_1", "gread_0_0",
+    "mmG_0_3_1", "mmF_0_0", "inter_1_1_1", "ttanh_0_0", "mmF_0_1", "mmF_0_2", "ttanh_0_1", "mmF_0_3",
+    "gread_0_1", "tT_0", "widen_2_0_2", "mmT_1_0", "quant_1_1", "widen_2_0_3", "mmG_1_0_0", "gread_0_2",
+    "ucopy_0", "mmG_1_1_0", "mmG_1_2_0", "phired_0", "widen_2_1_0", "mmG_1_3_0", "st_t0", "gread_0_3",
+    "mmG_1_0_1", "widen_2_1_1", "mmT_1_1", "inter_2_0_0", "mmG_1_1_1", "widen_2_1_2", "mmG_1_2_1", "mmG_1_3_1",
+    "gread_1_0", "bias_0", "mmF_1_0", "mmF_1_1", "ttanh_1_0", "mmF_1_2", "mmF_1_3", "inter_2_0_1",
+    "ttanh_1_1", "st_g0", "tT_1", "widen_2_1_3", "gread_1_1", "widen_3_0_0", "quant_2_0", "ucopy_1",
+    "gread_1_2", "widen_3_0_1", "mmT_2_0", "st_t1", "phired_1", "mmG_2_0_0", "widen_3_0_2", "mmG_2_1_0",
+    "gread_1_3", "mmG_2_2_0", "widen_3_0_3", "mmG_2_3_0", "inter_2_1_0", "widen_3_1_0", "bias_1", "inter_3_0_1",
+    "inter_2_1_1", "st_g1", "widen_3_1_1", "inter_3_0_0", "widen_3_1_2", "quant_2_1", "widen_3_1_3", "quant_3_0",
+    "mmG_2_0_1", "phit_0", "phit_1", "mmT_2_1", "inter_3_1_0", "st_p0", "mmG_2_1_1", "gread_2_0",
+    "st_p1", "mmG_2_2_1", "inter_3_1_1", "mmG_2_3_1", "ttanh_2_0", "mmF_2_0", "ttanh_2_1", "mmF_2_1",
+    "mmF_2_2", "gread_2_1", "mmF_2_3", "tT_2", "quant_3_1", "mmT_3_0", "ucopy_2", "mmG_3_0_0",
+    "gread_2_2", "mmG_3_1_0", "mmG_3_2_0", "phired_2", "st_t2", "mmG_3_3_0", "gread_2_3", "mmG_3_0_1",
+    "mmT_3_1", "mmG_3_1_1", "gread_3_0", "bias_2", "mmG_3_2_1", "mmG_3_3_1", "ttanh_3_0", "mmF_3_0",
+    "ttanh_3_1", "gread_3_1", "mmF_3_1", "mmF_3_2", "phit_2", "st_g2", "mmF_3_3", "tT_3",
+    "st_p2", "gread_3_2", "ucopy_3", "phired_3", "gread_3_3", "st_t3", "bias_3", "phit_3",
+    "st_g3", "st_p3",
 )
 
 
@@ -73,7 +75,11 @@ def tile_selfattention3d_pb_kernel(
         xbytes = {}
         wraw = {}
         bth = sb([P, 1], BF16, "bth")
-        bgp = sb([P, 640], BF16, "bgp")
+        brow = sb([P, 640], BF16, "brow")
+        ones = sb([P, P], BF16, "ones")
+        bgp = sb([P, 640], F32, "bgp")
+        nc.gpsimd.memset(brow[:], 0.0)
+        nc.gpsimd.memset(ones[:], 1.0)
 
         nc.scalar.dma_start(
             out=xsc[:].rearrange("p (g t) -> p g t", g=NPASS),
@@ -98,8 +104,8 @@ def tile_selfattention3d_pb_kernel(
                     nc.sync.dma_start(out=tl[:], in_=wg_rows[r - 2])
             else:
                 nc.sync.dma_start(out=bth[:], in_=b_theta.rearrange("(p o) -> p o", o=1))
-                nc.sync.dma_start(out=bgp[:, 0:512], in_=b_g.partition_broadcast(P))
-                nc.sync.dma_start(out=bgp[:, 512:640], in_=b_phi.partition_broadcast(P))
+                nc.sync.dma_start(out=brow[0:1, 0:512], in_=b_g.rearrange("(o n) -> o n", o=1))
+                nc.sync.dma_start(out=brow[0:1, 512:640], in_=b_phi.rearrange("(o n) -> o n", o=1))
 
         warm = sb([P, 1], F32, "warm")
         nc.vector.memset(warm[:], 0.0)
@@ -187,6 +193,22 @@ def tile_selfattention3d_pb_kernel(
             nc.vector.quantize_mx(
                 out=wc[g][:, lo:hi].bitcast(FP8X4), scales=wsc[g][:, lo:hi], in_=flat[:, 4 * lo:4 * hi]
             )
+
+        bbank = {}
+
+        def bmm():
+            bbank[0] = psum.tile([P, 512], F32, name="bias_g", tag="T", bufs=1)
+            bbank[1] = psum.tile([P, 4, P], F32, name="bias_phi", tag="U", bufs=1)
+            nc.tensor.matmul(out=bbank[0][:], lhsT=ones[:], rhs=brow[:, 0:512], start=True, stop=True)
+            nc.tensor.matmul(out=bbank[1][:, 0, :], lhsT=ones[:], rhs=brow[:, 512:640], start=True, stop=True)
+
+        def bcopy():
+            if V_BCOPY:
+                nc.vector.tensor_copy(out=bgp[:, 0:512], in_=bbank[0][:])
+                nc.vector.tensor_copy(out=bgp[:, 512:640], in_=bbank[1][:, 0, :])
+            else:
+                nc.scalar.copy(out=bgp[:, 0:512], in_=bbank[0][:])
+                nc.scalar.copy(out=bgp[:, 512:640], in_=bbank[1][:, 0, :])
 
         tbank = {}
         fbank = {}
@@ -286,7 +308,7 @@ def tile_selfattention3d_pb_kernel(
         fns = {
             "widen": widen, "flag": flag, "inter": inter, "quant": quant, "wT": wT, "wcopy": wcopy, "wq": wq,
             "mmT": mmT, "mmG": mmG, "mmF": mmF, "gread": gread, "phired": phired, "bias": bias, "phit": phit,
-            "ttanh": ttanh, "tT": tT, "ucopy": ucopy,
+            "ttanh": ttanh, "tT": tT, "ucopy": ucopy, "bmm": bmm, "bcopy": bcopy,
         }
         for item in ORDER:
             parts = item.split("_")

@@ -20,39 +20,9 @@ NCHUNK = 4
 NPASS = 2
 CL = 512
 
-V_WIDEN = ((0, 0, 1), (0, 0, 2), (0, 0, 3), (0, 1, 2), (1, 0, 1), (1, 0, 3), (1, 1, 0))
-S_INTER = ((3, 0, 1),)
-G_INTER = {}
-V_WCOPY = ()
-V_UCOPY = ()
-V_BCOPY = False
-LOADS = ('x00', 'x01', 'bias', 'w0', 'w1', 'x10', 'w2', 'w3', 'w4', 'w5', 'x11', 'x20', 'x21', 'x30', 'x31')
-ORDER = (
-    "widen_0_0_0", "widen_0_0_1", "widen_0_0_2", "widen_0_0_3", "widen_0_1_0", "widen_0_1_2", "inter_0_0_0", "widen_0_1_1",
-    "inter_0_0_1", "widen_0_1_3", "wT_0_0", "wT_0_1", "quant_0_0", "wcopy_0_0", "bmm", "inter_0_1_0",
-    "wcopy_0_1", "wq_0_0", "bcopy", "wT_1_0", "inter_0_1_1", "widen_1_0_0", "wT_1_1", "wq_1_0",
-    "wcopy_1_0", "quant_0_1", "wT_2_0", "wcopy_1_1", "widen_1_0_1", "wT_2_1", "widen_1_0_3", "widen_1_0_2",
-    "widen_1_1_0", "mmT_0_0", "wcopy_2_0", "inter_1_0_0", "wcopy_2_1", "wq_0_1", "widen_1_1_1", "wq_1_1",
-    "widen_1_1_2", "mmG_0_0_0", "mmG_0_1_0", "inter_1_0_1", "widen_1_1_3", "mmG_0_2_0", "mmG_0_3_0", "widen_2_0_0",
-    "mmG_0_0_1", "inter_1_1_0", "mmT_0_1", "widen_2_0_1", "mmG_0_1_1", "quant_1_0", "mmG_0_2_1", "gread_0_0",
-    "mmG_0_3_1", "mmF_0_0", "inter_1_1_1", "ttanh_0_0", "mmF_0_1", "mmF_0_2", "ttanh_0_1", "mmF_0_3",
-    "gread_0_1", "tT_0", "widen_2_0_2", "mmT_1_0", "quant_1_1", "widen_2_0_3", "mmG_1_0_0", "gread_0_2",
-    "ucopy_0", "mmG_1_1_0", "mmG_1_2_0", "phired_0", "widen_2_1_0", "mmG_1_3_0", "st_t0", "gread_0_3",
-    "mmG_1_0_1", "widen_2_1_1", "mmT_1_1", "inter_2_0_0", "mmG_1_1_1", "widen_2_1_2", "mmG_1_2_1", "mmG_1_3_1",
-    "gread_1_0", "bias_0", "mmF_1_0", "mmF_1_1", "ttanh_1_0", "mmF_1_2", "mmF_1_3", "inter_2_0_1",
-    "ttanh_1_1", "st_g0", "tT_1", "widen_2_1_3", "gread_1_1", "widen_3_0_0", "quant_2_0", "ucopy_1",
-    "gread_1_2", "widen_3_0_1", "mmT_2_0", "st_t1", "phired_1", "mmG_2_0_0", "widen_3_0_2", "mmG_2_1_0",
-    "gread_1_3", "mmG_2_2_0", "widen_3_0_3", "mmG_2_3_0", "inter_2_1_0", "widen_3_1_0", "bias_1", "inter_3_0_1",
-    "inter_2_1_1", "st_g1", "widen_3_1_1", "inter_3_0_0", "widen_3_1_2", "quant_2_1", "widen_3_1_3", "quant_3_0",
-    "mmG_2_0_1", "phit_0", "phit_1", "mmT_2_1", "inter_3_1_0", "st_p0", "mmG_2_1_1", "gread_2_0",
-    "st_p1", "mmG_2_2_1", "inter_3_1_1", "mmG_2_3_1", "ttanh_2_0", "mmF_2_0", "ttanh_2_1", "mmF_2_1",
-    "mmF_2_2", "gread_2_1", "mmF_2_3", "tT_2", "quant_3_1", "mmT_3_0", "ucopy_2", "mmG_3_0_0",
-    "gread_2_2", "mmG_3_1_0", "mmG_3_2_0", "phired_2", "st_t2", "mmG_3_3_0", "gread_2_3", "mmG_3_0_1",
-    "mmT_3_1", "mmG_3_1_1", "gread_3_0", "bias_2", "mmG_3_2_1", "mmG_3_3_1", "ttanh_3_0", "mmF_3_0",
-    "ttanh_3_1", "gread_3_1", "mmF_3_1", "mmF_3_2", "phit_2", "st_g2", "mmF_3_3", "tT_3",
-    "st_p2", "gread_3_2", "ucopy_3", "phired_3", "gread_3_3", "st_t3", "bias_3", "phit_3",
-    "st_g3", "st_p3",
-)
+V_WIDEN = ((0, 0),)
+W_COPY_ON_SCALAR = (True, True, True, True, True, True)
+U_COPY_ON_SCALAR = True
 
 
 def tile_selfattention3d_pb_kernel(
@@ -61,258 +31,240 @@ def tile_selfattention3d_pb_kernel(
     nc = tc.nc
     with ExitStack() as ctx:
         keep = ctx.enter_context(tc.tile_pool(name="keep", bufs=1))
+        work = ctx.enter_context(tc.tile_pool(name="work", bufs=2))
         psum = ctx.enter_context(tc.psum_pool(name="psum", bufs=1))
-        ctx.enter_context(tc.manual_schedule())
 
-        def sb(shape, dtype, name, align=None):
-            if align is None:
-                return keep.tile(shape, dtype, name=name, tag=name)
-            return keep.tile(shape, dtype, name=name, tag=name, align_bytes=align)
-
-        xsc = sb([P, 8], F32, "xsc")
-        xb = x_bytes[0].rearrange("(g p t) f i j -> g p t (f i j)", g=NPASS, p=P, t=4)
-        wg_rows = w_g.rearrange("(r p) k -> r p k", p=P)
-        xbytes = {}
-        wraw = {}
-        bth = sb([P, 1], BF16, "bth")
-        brow = sb([P, 640], BF16, "brow")
-        ones = sb([P, P], BF16, "ones")
-        bgp = sb([P, 640], F32, "bgp")
-        nc.gpsimd.memset(brow[:], 0.0)
-        nc.gpsimd.memset(ones[:], 1.0)
-
-        nc.scalar.dma_start(
+        xsc = keep.tile([P, 8], F32, name="xsc", tag="xsc")
+        nc.sync.dma_start(
             out=xsc[:].rearrange("p (g t) -> p g t", g=NPASS),
             in_=x_scale.rearrange("o k a b c -> (o k a b c)").rearrange("(g p t) -> p g t", g=NPASS, p=P, t=4),
         )
-        for nm in LOADS:
-            if nm[0] == "x":
-                c = int(nm[1])
-                g = int(nm[2])
-                tl = sb([P, 4, CL], U8, "xbytes_%d_%d" % (c, g))
-                nc.sync.dma_start(out=tl[:], in_=xb[g][:, :, c * CL:(c + 1) * CL])
-                xbytes[(c, g)] = tl
-            elif nm[0] == "w":
-                r = int(nm[1])
-                tl = sb([P, 1024], BF16, "wraw%d" % r)
-                wraw[r] = tl
-                if r == 0:
-                    nc.sync.dma_start(out=tl[:], in_=w_theta)
-                elif r == 1:
-                    nc.sync.dma_start(out=tl[:], in_=w_phi)
-                else:
-                    nc.sync.dma_start(out=tl[:], in_=wg_rows[r - 2])
-            else:
-                nc.sync.dma_start(out=bth[:], in_=b_theta.rearrange("(p o) -> p o", o=1))
-                nc.sync.dma_start(out=brow[0:1, 0:512], in_=b_g.rearrange("(o n) -> o n", o=1))
-                nc.sync.dma_start(out=brow[0:1, 512:640], in_=b_phi.rearrange("(o n) -> o n", o=1))
+        xb = x_bytes[0].rearrange("(g p t) f i j -> g p t (f i j)", g=NPASS, p=P, t=4)
+        xbytes = {}
 
-        warm = sb([P, 1], F32, "warm")
+        def load_x(c, g):
+            tl = keep.tile([P, 4, CL], U8, name="xbytes_%d_%d" % (c, g), tag="xbytes_%d_%d" % (c, g))
+            nc.sync.dma_start(out=tl[:], in_=xb[g][:, :, c * CL:(c + 1) * CL])
+            xbytes[(c, g)] = tl
+
+        wraw = []
+        for r in range(6):
+            wraw.append(keep.tile([P, 1024], BF16, name="wraw%d" % r, tag="wraw%d" % r))
+        wg_rows = w_g.rearrange("(r p) k -> r p k", p=P)
+
+        load_x(0, 0)
+        load_x(0, 1)
+        nc.sync.dma_start(out=wraw[0][:], in_=w_theta)
+        nc.sync.dma_start(out=wraw[1][:], in_=w_phi)
+        load_x(1, 0)
+        nc.sync.dma_start(out=wraw[2][:], in_=wg_rows[0])
+        nc.sync.dma_start(out=wraw[3][:], in_=wg_rows[1])
+        load_x(1, 1)
+        nc.sync.dma_start(out=wraw[4][:], in_=wg_rows[2])
+        nc.sync.dma_start(out=wraw[5][:], in_=wg_rows[3])
+        bth = keep.tile([P, 1], BF16, name="bth", tag="bth")
+        nc.sync.dma_start(out=bth[:], in_=b_theta.rearrange("(p o) -> p o", o=1))
+        bphi = keep.tile([P, 128], BF16, name="bphi", tag="bphi")
+        nc.sync.dma_start(out=bphi[:], in_=b_phi.partition_broadcast(P))
+        bg = keep.tile([P, 512], BF16, name="bg", tag="bg")
+        nc.sync.dma_start(out=bg[:], in_=b_g.partition_broadcast(P))
+        for c in range(2, NCHUNK):
+            for g in range(NPASS):
+                load_x(c, g)
+
+
+        warm = keep.tile([P, 1], F32, name="warm", tag="warm")
         nc.vector.memset(warm[:], 0.0)
-        warm2 = sb([P, 1], F32, "warm2")
+        warm2 = keep.tile([P, 1], F32, name="warm2", tag="warm2")
         nc.scalar.activation(out=warm2[:], in_=warm[:], func=ACT.Tanh)
 
-        ident = sb([P, P], F32, "ident")
+        ident = keep.tile([P, P], F32, name="ident", tag="ident")
         make_identity(nc, ident[:])
 
         wide = {}
         grp = {}
         xc = {}
         xs = {}
-        flags = {}
-        for c in range(NCHUNK):
-            for g in range(NPASS):
-                wide[(c, g)] = sb([P, 4, CL], BF16, "wide_%d_%d" % (c, g))
-                grp[(c, g)] = sb([P, CL, 4], BF16, "grp_%d_%d" % (c, g), 64)
-                xc[(c, g)] = sb([P, CL], U32, "xc_%d_%d" % (c, g), 64)
-                xs[(c, g)] = sb([P, CL], U8, "xs_%d_%d" % (c, g), 64)
 
-        def widen(c, g, t):
-            col = xsc[:, 4 * g + t:4 * g + t + 1]
-            dst = wide[(c, g)][:, t, :]
-            src = xbytes[(c, g)][:, t, :].bitcast(FP8)
-            if (c, g, t) in V_WIDEN:
-                nc.vector.tensor_scalar(out=dst, in0=src, scalar1=col, scalar2=None, op0=ALU.mult)
-            else:
-                nc.scalar.activation(out=dst, in_=src, func=ACT.Copy, scale=col)
-
-        def flag(c):
-            flags[c] = sb([P, 1], F32, "flag_%d" % c)
-            nc.vector.memset(flags[c][:], 1.0)
-
-        def inter(c, g, di):
-            src = wide[(c, g)][:].rearrange("p t (a di j dj) -> p di dj a j t", a=16, di=2, j=8, dj=2)
-            dst = grp[(c, g)][:].rearrange("p (di dj a j) t -> p di dj a j t", di=2, dj=2, a=16, j=8)
-            if (c, g, di) in S_INTER:
-                for dj in range(2):
-                    nc.scalar.copy(out=dst[:, di, dj], in_=src[:, di, dj])
-            elif (c, g, di) in G_INTER:
-                one = flags[G_INTER[(c, g, di)]]
-                for dj in range(2):
-                    nc.gpsimd.tensor_scalar(
-                        out=dst[:, di, dj], in0=src[:, di, dj], scalar1=one[:, 0:1], scalar2=0.0,
-                        op0=ALU.mult, op1=ALU.add,
+        def widen(c, g):
+            wd = work.tile([P, 4, CL], BF16, name="wide_%d_%d" % (c, g), tag="wide", bufs=4)
+            wide[(c, g)] = wd
+            src = xbytes[(c, g)]
+            for t in range(4):
+                col = xsc[:, 4 * g + t:4 * g + t + 1]
+                if (c, g) in V_WIDEN:
+                    nc.vector.tensor_scalar(
+                        out=wd[:, t, :], in0=src[:, t, :].bitcast(FP8), scalar1=col, scalar2=None, op0=ALU.mult
                     )
-            else:
+                else:
+                    nc.scalar.activation(out=wd[:, t, :], in_=src[:, t, :].bitcast(FP8), func=ACT.Copy, scale=col)
+
+        def inter(c, g):
+            gr = work.tile([P, CL, 4], BF16, name="grp_%d_%d" % (c, g), tag="grp", bufs=3, align_bytes=64)
+            grp[(c, g)] = gr
+            src = wide[(c, g)][:].rearrange("p t (a di j dj) -> p di a j dj t", a=16, di=2, j=8, dj=2)
+            dst = gr[:].rearrange("p (di dj a j) t -> p di a j dj t", di=2, dj=2, a=16, j=8)
+            for di in range(2):
                 nc.vector.tensor_copy(out=dst[:, di], in_=src[:, di])
 
         def quant(c, g):
+            cd = keep.tile([P, CL], U32, name="xc_%d_%d" % (c, g), tag="xc_%d_%d" % (c, g), align_bytes=64)
+            sc = keep.tile([P, CL], U8, name="xs_%d_%d" % (c, g), tag="xs_%d_%d" % (c, g), align_bytes=64)
+            xc[(c, g)] = cd
+            xs[(c, g)] = sc
             nc.vector.quantize_mx(
-                out=xc[(c, g)][:].bitcast(FP8X4), scales=xs[(c, g)][:], in_=grp[(c, g)][:].rearrange("p n t -> p (n t)")
+                out=cd[:].bitcast(FP8X4), scales=sc[:], in_=grp[(c, g)][:].rearrange("p n t -> p (n t)")
             )
 
         wgrp = []
         wc = []
         wsc = []
         for g in range(NPASS):
-            wgrp.append(sb([P, 768, 4], BF16, "wgrp%d" % g, 64))
-            wc.append(sb([P, 768], U32, "wc%d" % g, 64))
-            wsc.append(sb([P, 768], U8, "wsc%d" % g, 64))
-        wbank = {}
+            wgrp.append(keep.tile([P, 768, 4], BF16, name="wgrp%d" % g, tag="wgrp%d" % g, align_bytes=64))
+            wc.append(keep.tile([P, 768], U32, name="wc%d" % g, tag="wc%d" % g, align_bytes=64))
+            wsc.append(keep.tile([P, 768], U8, name="wsc%d" % g, tag="wsc%d" % g, align_bytes=64))
 
-        def wT(q, g):
+        def wprep(q, g):
             bank = psum.tile([P, 2, 2, P], F32, name="wt_%d_%d" % (q, g), tag="G", bufs=5)
-            wbank[(q, g)] = bank
             for r in range(2):
                 words = wraw[2 * q + r][:].bitcast(F32)
                 for u in range(2):
                     nc.tensor.transpose(bank[:, r, u, :], words[:, 256 * g + u:256 * (g + 1):2], ident[:])
-
-        def wcopy(q, g):
             dst = wgrp[g][:].rearrange("p o t -> p (o t)").bitcast(F32)[:, 512 * q:512 * (q + 1)]
             dst = dst.rearrange("p (r o u) -> p r o u", r=2, o=P, u=2)
-            src = wbank[(q, g)][:].rearrange("p r u o -> p r o u")
-            if (q, g) in V_WCOPY:
-                nc.vector.tensor_copy(out=dst, in_=src)
-            else:
+            src = bank[:].rearrange("p r u o -> p r o u")
+            if W_COPY_ON_SCALAR[2 * q + g]:
                 nc.scalar.copy(out=dst, in_=src)
+            else:
+                nc.vector.tensor_copy(out=dst, in_=src)
 
-        def wq(g, part):
-            lo, hi = ((0, 256), (256, 768))[part]
+        def wquant(g, lo, hi):
             flat = wgrp[g][:].rearrange("p o t -> p (o t)")
             nc.vector.quantize_mx(
                 out=wc[g][:, lo:hi].bitcast(FP8X4), scales=wsc[g][:, lo:hi], in_=flat[:, 4 * lo:4 * hi]
             )
 
-        bbank = {}
-
-        def bmm():
-            bbank[0] = psum.tile([P, 512], F32, name="bias_g", tag="T", bufs=1)
-            bbank[1] = psum.tile([P, 4, P], F32, name="bias_phi", tag="U", bufs=1)
-            nc.tensor.matmul(out=bbank[0][:], lhsT=ones[:], rhs=brow[:, 0:512], start=True, stop=True)
-            nc.tensor.matmul(out=bbank[1][:, 0, :], lhsT=ones[:], rhs=brow[:, 512:640], start=True, stop=True)
-
-        def bcopy():
-            if V_BCOPY:
-                nc.vector.tensor_copy(out=bgp[:, 0:512], in_=bbank[0][:])
-                nc.vector.tensor_copy(out=bgp[:, 512:640], in_=bbank[1][:, 0, :])
-            else:
-                nc.scalar.copy(out=bgp[:, 0:512], in_=bbank[0][:])
-                nc.scalar.copy(out=bgp[:, 512:640], in_=bbank[1][:, 0, :])
-
         tbank = {}
         fbank = {}
         gbank = {}
 
-        def mmT(c, g):
-            if g == 0:
-                tbank[c] = psum.tile([P, CL], F32, name="T_%d" % c, tag="T", bufs=1)
-            nc.tensor.matmul_mx(
-                out=tbank[c][:],
-                lhsT=wc[g][:, 0:128].bitcast(FP8X4), lhsT_scale=wsc[g][:, 0:128],
-                rhs=xc[(c, g)][:].bitcast(FP8X4), rhs_scale=xs[(c, g)][:],
-                start=(g == 0), stop=(g == NPASS - 1),
-            )
-
-        def mmG(c, w, g):
-            if g == 0:
-                gbank[(c, w)] = psum.tile([P, 512], F32, name="G_%d_%d" % (c, w), tag="G", bufs=5)
-            cols = slice(P * w, P * (w + 1))
-            nc.tensor.matmul_mx(
-                out=gbank[(c, w)][:],
-                lhsT=xc[(c, g)][:, cols].bitcast(FP8X4), lhsT_scale=xs[(c, g)][:, cols],
-                rhs=wc[g][:, 256:768].bitcast(FP8X4), rhs_scale=wsc[g][:, 256:768],
-                start=(g == 0), stop=(g == NPASS - 1),
-            )
-
-        def mmF(c, w):
-            if w == 0:
-                fbank[c] = psum.tile([P, 4, P], F32, name="F_%d" % c, tag="F", bufs=1)
-            cols = slice(P * w, P * (w + 1))
+        def mm_theta(c):
+            tb = psum.tile([P, CL], F32, name="T_%d" % c, tag="T", bufs=1)
+            tbank[c] = tb
             for g in range(NPASS):
                 nc.tensor.matmul_mx(
-                    out=fbank[c][:, w, :],
-                    lhsT=xc[(c, g)][:, cols].bitcast(FP8X4), lhsT_scale=xs[(c, g)][:, cols],
+                    out=tb[:],
+                    lhsT=wc[g][:, 0:128].bitcast(FP8X4), lhsT_scale=wsc[g][:, 0:128],
+                    rhs=xc[(c, g)][:].bitcast(FP8X4), rhs_scale=xs[(c, g)][:],
+                    start=(g == 0), stop=(g == NPASS - 1),
+                )
+
+        def mm_tile(c, w):
+            if w == 0:
+                fbank[c] = psum.tile([P, 4, P], F32, name="F_%d" % c, tag="F", bufs=1)
+            gb = psum.tile([P, 512], F32, name="G_%d_%d" % (c, w), tag="G", bufs=5)
+            gbank[(c, w)] = gb
+            cols = slice(P * w, P * (w + 1))
+            for g in range(NPASS):
+                lhsT = xc[(c, g)][:, cols].bitcast(FP8X4)
+                lsc = xs[(c, g)][:, cols]
+                nc.tensor.matmul_mx(
+                    out=gb[:], lhsT=lhsT, lhsT_scale=lsc,
+                    rhs=wc[g][:, 256:768].bitcast(FP8X4), rhs_scale=wsc[g][:, 256:768],
+                    start=(g == 0), stop=(g == NPASS - 1),
+                )
+                nc.tensor.matmul_mx(
+                    out=fbank[c][:, w, :], lhsT=lhsT, lhsT_scale=lsc,
                     rhs=wc[g][:, 128:256].bitcast(FP8X4), rhs_scale=wsc[g][:, 128:256],
                     start=(g == 0), stop=(g == NPASS - 1),
                 )
 
         acc = {}
-        gp = {}
-        po = {}
+
+        def g_first(c):
+            acc[c] = work.tile([P, 512], F32, name="acc_%d" % c, tag="acc", bufs=2)
+            nc.scalar.copy(out=acc[c][:], in_=gbank[(c, 0)][:])
+
+        def g_max(c, w):
+            nc.vector.tensor_tensor(out=acc[c][:], in0=gbank[(c, w)][:], in1=acc[c][:], op=ALU.max)
+
+        def g_last(c):
+            go = work.tile([P, 512], F32, name="gout_%d" % c, tag="gout", bufs=2)
+            nc.vector.tensor_tensor(out=go[:], in0=acc[c][:], in1=bg[:], op=ALU.add)
+            nc.sync.dma_start(out=out_2[0, P * c:P * (c + 1), :], in_=go[:])
+
+        def phi_all(c):
+            pr = work.tile([P, P], F32, name="pr_%d" % c, tag="pr", bufs=2)
+            nc.vector.tensor_reduce(out=pr[:], in_=fbank[c][:].rearrange("p w k -> p k w"), axis=AX.X, op=ALU.max)
+            pb = work.tile([P, P], F32, name="pb_%d" % c, tag="pb", bufs=2)
+            nc.vector.tensor_tensor(out=pb[:], in0=pr[:], in1=bphi[:], op=ALU.add)
+            po = work.tile([P, P], F32, name="po_%d" % c, tag="po", bufs=2)
+            nc.scalar.activation(out=po[:], in_=pb[:], func=ACT.Tanh)
+            nc.sync.dma_start(out=out_1[0, P * c:P * (c + 1), :], in_=po[:])
+
         th = {}
-        tho = {}
-        ubank = {}
-        for c in range(NCHUNK):
-            acc[c] = sb([P, 640], F32, "acc_%d" % c)
-            gp[c] = sb([P, 640], F32, "gp_%d" % c)
-            po[c] = sb([P, P], F32, "po_%d" % c)
-            th[c] = sb([P, CL], F32, "th_%d" % c)
-            tho[c] = sb([P, 4, P], F32, "tho_%d" % c)
 
-        def gread(c, w):
-            if w == 0:
-                nc.scalar.copy(out=acc[c][:, 0:512], in_=gbank[(c, 0)][:])
-            else:
-                nc.vector.tensor_tensor(out=acc[c][:, 0:512], in0=gbank[(c, w)][:], in1=acc[c][:, 0:512], op=ALU.max)
-
-        def phired(c):
-            nc.vector.tensor_reduce(
-                out=acc[c][:, 512:640], in_=fbank[c][:].rearrange("p w k -> p k w"), axis=AX.X, op=ALU.max
-            )
-
-        def bias(c):
-            nc.vector.tensor_tensor(out=gp[c][:], in0=acc[c][:], in1=bgp[:], op=ALU.add)
-
-        def phit(c):
-            nc.scalar.activation(out=po[c][:], in_=gp[c][:, 512:640], func=ACT.Tanh)
-
-        def ttanh(c, dj):
+        def theta_tanh(c):
+            th[c] = work.tile([P, CL], F32, name="th_%d" % c, tag="th", bufs=2)
             src = tbank[c][:].rearrange("p (di dj a j) -> p dj a di j", di=2, dj=2, a=16, j=8)
             dst = th[c][:].rearrange("p (dj a di j) -> p dj a di j", dj=2, a=16, di=2, j=8)
-            nc.scalar.activation(out=dst[:, dj], in_=src[:, dj], func=ACT.Tanh, bias=bth[:, 0:1])
-
-        def tT(c):
-            ubank[c] = psum.tile([P, 4, P], F32, name="U_%d" % c, tag="U", bufs=1)
             for dj in range(2):
-                for f in range(2):
-                    b = 2 * dj + f
-                    nc.tensor.transpose(ubank[c][:, 2 * f + dj, :], th[c][:, P * b:P * (b + 1)], ident[:])
-
-        def ucopy(c):
-            if c in V_UCOPY:
-                nc.vector.tensor_copy(out=tho[c][:], in_=ubank[c][:])
-            else:
-                nc.scalar.copy(out=tho[c][:], in_=ubank[c][:])
+                nc.scalar.activation(out=dst[:, dj], in_=src[:, dj], func=ACT.Tanh, bias=bth[:, 0:1])
 
         out0v = out_0[0].rearrange("(c f p dj) k -> c p f (dj k)", c=NCHUNK, f=2, p=P, dj=2)
 
-        def st(kind, c):
-            if kind == "g":
-                nc.sync.dma_start(out=out_2[0, P * c:P * (c + 1), :], in_=gp[c][:, 0:512])
-            elif kind == "p":
-                nc.sync.dma_start(out=out_1[0, P * c:P * (c + 1), :], in_=po[c][:])
+        def theta_out(c):
+            ub = psum.tile([P, 4, P], F32, name="U_%d" % c, tag="U", bufs=1)
+            for dj in range(2):
+                for f in range(2):
+                    b = 2 * dj + f
+                    nc.tensor.transpose(ub[:, 2 * f + dj, :], th[c][:, P * b:P * (b + 1)], ident[:])
+            to = work.tile([P, 4, P], F32, name="tho_%d" % c, tag="tho", bufs=2)
+            if U_COPY_ON_SCALAR:
+                nc.scalar.copy(out=to[:], in_=ub[:])
             else:
-                nc.sync.dma_start(out=out0v[c], in_=tho[c][:].rearrange("p (f dj) k -> p f (dj k)", f=2))
+                nc.vector.tensor_copy(out=to[:], in_=ub[:])
+            nc.sync.dma_start(out=out0v[c], in_=to[:].rearrange("p (f dj) k -> p f (dj k)", f=2))
 
-        fns = {
-            "widen": widen, "flag": flag, "inter": inter, "quant": quant, "wT": wT, "wcopy": wcopy, "wq": wq,
-            "mmT": mmT, "mmG": mmG, "mmF": mmF, "gread": gread, "phired": phired, "bias": bias, "phit": phit,
-            "ttanh": ttanh, "tT": tT, "ucopy": ucopy, "bmm": bmm, "bcopy": bcopy,
-        }
-        for item in ORDER:
-            parts = item.split("_")
-            if parts[0] == "st":
-                st(parts[1][0], int(parts[1][1]))
-            else:
-                fns[parts[0]](*[int(v) for v in parts[1:]])
+        widen(0, 0)
+        widen(0, 1)
+        inter(0, 0)
+        wprep(0, 0)
+        wprep(0, 1)
+        quant(0, 0)
+        inter(0, 1)
+        wprep(1, 0)
+        wprep(1, 1)
+        quant(0, 1)
+        wprep(2, 0)
+        wprep(2, 1)
+        widen(1, 0)
+        for g in range(NPASS):
+            wquant(g, 0, 256)
+            wquant(g, 256, 768)
+        widen(1, 1)
+
+        for c in range(NCHUNK):
+            nxt = c + 1 < NCHUNK
+            mm_theta(c)
+            for w in range(4):
+                mm_tile(c, w)
+            if nxt:
+                inter(c + 1, 0)
+            if c + 2 < NCHUNK:
+                widen(c + 2, 0)
+            theta_tanh(c)
+            g_first(c)
+            g_max(c, 1)
+            if nxt:
+                quant(c + 1, 0)
+                inter(c + 1, 1)
+            theta_out(c)
+            g_max(c, 2)
+            if nxt:
+                quant(c + 1, 1)
+            g_max(c, 3)
+            if c + 2 < NCHUNK:
+                widen(c + 2, 1)
+            phi_all(c)
+            g_last(c)

@@ -23,6 +23,7 @@ CL = 512
 V_WIDEN = ((0, 0),)
 W_COPY_ON_SCALAR = (True, True, True, True, True, True)
 U_COPY_ON_SCALAR = True
+G_BIAS = (2,)
 
 
 def tile_selfattention3d_pb_kernel(
@@ -190,14 +191,14 @@ def tile_selfattention3d_pb_kernel(
 
         def g_last(c):
             go = work.tile([P, 512], F32, name="gout_%d" % c, tag="gout", bufs=2)
-            nc.vector.tensor_tensor(out=go[:], in0=acc[c][:], in1=bg[:], op=ALU.add)
+            (nc.gpsimd if c in G_BIAS else nc.vector).tensor_tensor(out=go[:], in0=acc[c][:], in1=bg[:], op=ALU.add)
             nc.sync.dma_start(out=out_2[0, P * c:P * (c + 1), :], in_=go[:])
 
         def phi_all(c):
             pr = work.tile([P, P], F32, name="pr_%d" % c, tag="pr", bufs=2)
             nc.vector.tensor_reduce(out=pr[:], in_=fbank[c][:].rearrange("p w k -> p k w"), axis=AX.X, op=ALU.max)
             pb = work.tile([P, P], F32, name="pb_%d" % c, tag="pb", bufs=2)
-            nc.vector.tensor_tensor(out=pb[:], in0=pr[:], in1=bphi[:], op=ALU.add)
+            (nc.gpsimd if c in G_BIAS else nc.vector).tensor_tensor(out=pb[:], in0=pr[:], in1=bphi[:], op=ALU.add)
             po = work.tile([P, P], F32, name="po_%d" % c, tag="po", bufs=2)
             nc.scalar.activation(out=po[:], in_=pb[:], func=ACT.Tanh)
             nc.sync.dma_start(out=out_1[0, P * c:P * (c + 1), :], in_=po[:])

@@ -103,8 +103,8 @@ def tile_selfattention3d_pb_kernel(
         def inter(c, g):
             gr = work.tile([P, CL, 4], BF16, name="grp_%d_%d" % (c, g), tag="grp", bufs=3, align_bytes=64)
             grp[(c, g)] = gr
-            src = wide[(c, g)][:].rearrange("p t (a di j dj) -> p di a j dj t", a=16, di=2, j=8, dj=2)
-            dst = gr[:].rearrange("p (di dj a j) t -> p di a j dj t", di=2, dj=2, a=16, j=8)
+            src = wide[(c, g)][:].rearrange("p t (a di j b dj) -> p di a j t b dj", a=16, di=2, j=4, b=2, dj=2)
+            dst = gr[:].rearrange("p (di dj a j b) t -> p di a j t b dj", di=2, dj=2, a=16, j=4, b=2)
             for di in range(2):
                 nc.vector.tensor_copy(out=dst[:, di], in_=src[:, di])
 

@@ -100,21 +100,25 @@ def tile_selfattention3d_pb_kernel(
                 else:
                     nc.scalar.activation(out=wd[:, t, :], in_=src[:, t, :].bitcast(FP8), func=ACT.Copy, scale=col)
 
-        def inter(c, g):
-            gr = work.tile([P, CL, 4], BF16, name="grp_%d_%d" % (c, g), tag="grp", bufs=3, align_bytes=64)
-            grp[(c, g)] = gr
+        def inter_half(c, g, di):
+            if di == 0:
+                grp[(c, g)] = work.tile([P, CL, 4], BF16, name="grp_%d_%d" % (c, g), tag="grp", bufs=3, align_bytes=64)
+            gr = grp[(c, g)]
             src = wide[(c, g)][:].rearrange("p t (a di j b dj) -> p di a j t b dj", a=16, di=2, j=4, b=2, dj=2)
             dst = gr[:].rearrange("p (di dj a j b) t -> p di a j t b dj", di=2, dj=2, a=16, j=4, b=2)
-            for di in range(2):
-                nc.vector.tensor_copy(out=dst[:, di], in_=src[:, di])
+            nc.vector.tensor_copy(out=dst[:, di], in_=src[:, di])
 
-        def quant(c, g):
-            cd = keep.tile([P, CL], U32, name="xc_%d_%d" % (c, g), tag="xc_%d_%d" % (c, g), align_bytes=64)
-            sc = keep.tile([P, CL], U8, name="xs_%d_%d" % (c, g), tag="xs_%d_%d" % (c, g), align_bytes=64)
-            xc[(c, g)] = cd
-            xs[(c, g)] = sc
+        def inter(c, g):
+            for di in range(2):
+                inter_half(c, g, di)
+
+        def quant(c, g, lo=0, hi=CL):
+            if lo == 0:
+                xc[(c, g)] = keep.tile([P, CL], U32, name="xc_%d_%d" % (c, g), tag="xc_%d_%d" % (c, g), align_bytes=64)
+                xs[(c, g)] = keep.tile([P, CL], U8, name="xs_%d_%d" % (c, g), tag="xs_%d_%d" % (c, g), align_bytes=64)
+            flat = grp[(c, g)][:].rearrange("p n t -> p (n t)")
             nc.vector.quantize_mx(
-                out=cd[:].bitcast(FP8X4), scales=sc[:], in_=grp[(c, g)][:].rearrange("p n t -> p (n t)")
+                out=xc[(c, g)][:, lo:hi].bitcast(FP8X4), scales=xs[(c, g)][:, lo:hi], in_=flat[:, 4 * lo:4 * hi]
             )
 
         wgrp = []
@@ -149,14 +153,14 @@ def tile_selfattention3d_pb_kernel(
         fbank = {}
         gbank = {}
 
-        def mm_theta(c):
-            tb = psum.tile([P, CL], F32, name="T_%d" % c, tag="T", bufs=1)
-            tbank[c] = tb
+        def mm_theta(c, lo=0, hi=CL):
+            if lo == 0:
+                tbank[c] = psum.tile([P, CL], F32, name="T_%d" % c, tag="T", bufs=1)
             for g in range(NPASS):
                 nc.tensor.matmul_mx(
-                    out=tb[:],
+                    out=tbank[c][:, lo:hi],
                     lhsT=wc[g][:, 0:128].bitcast(FP8X4), lhsT_scale=wsc[g][:, 0:128],
-                    rhs=xc[(c, g)][:].bitcast(FP8X4), rhs_scale=xs[(c, g)][:],
+                    rhs=xc[(c, g)][:, lo:hi].bitcast(FP8X4), rhs_scale=xs[(c, g)][:, lo:hi],
                     start=(g == 0), stop=(g == NPASS - 1),
                 )
 
@@ -189,28 +193,42 @@ def tile_selfattention3d_pb_kernel(
         def g_max(c, w):
             nc.vector.tensor_tensor(out=acc[c][:], in0=gbank[(c, w)][:], in1=acc[c][:], op=ALU.max)
 
-        def g_last(c):
-            go = work.tile([P, 512], F32, name="gout_%d" % c, tag="gout", bufs=2)
-            (nc.gpsimd if c in G_BIAS else nc.vector).tensor_tensor(out=go[:], in0=acc[c][:], in1=bg[:], op=ALU.add)
-            nc.sync.dma_start(out=out_2[0, P * c:P * (c + 1), :], in_=go[:])
+        gout = {}
 
-        def phi_all(c):
-            pr = work.tile([P, P], F32, name="pr_%d" % c, tag="pr", bufs=2)
-            nc.vector.tensor_reduce(out=pr[:], in_=fbank[c][:].rearrange("p w k -> p k w"), axis=AX.X, op=ALU.max)
+        def g_bias(c, engine, lo, hi):
+            if lo == 0:
+                gout[c] = work.tile([P, 512], F32, name="gout_%d" % c, tag="gout", bufs=2)
+            engine.tensor_tensor(out=gout[c][:, lo:hi], in0=acc[c][:, lo:hi], in1=bg[:, lo:hi], op=ALU.add)
+
+        def g_store(c, lo, hi):
+            nc.sync.dma_start(out=out_2[0, P * c:P * (c + 1), lo:hi], in_=gout[c][:, lo:hi])
+
+        def g_last(c):
+            g_bias(c, nc.gpsimd if c in G_BIAS else nc.vector, 0, 512)
+            g_store(c, 0, 512)
+
+        pooled = {}
+
+        def phi_pool(c):
+            pooled[c] = work.tile([P, P], F32, name="pr_%d" % c, tag="pr", bufs=2)
+            nc.vector.tensor_reduce(out=pooled[c][:], in_=fbank[c][:].rearrange("p w k -> p k w"), axis=AX.X, op=ALU.max)
+
+        def phi_last(c):
+            pr = pooled[c]
             pb = work.tile([P, P], F32, name="pb_%d" % c, tag="pb", bufs=2)
-            (nc.gpsimd if c in G_BIAS else nc.vector).tensor_tensor(out=pb[:], in0=pr[:], in1=bphi[:], op=ALU.add)
+            nc.vector.tensor_tensor(out=pb[:], in0=pr[:], in1=bphi[:], op=ALU.add)
             po = work.tile([P, P], F32, name="po_%d" % c, tag="po", bufs=2)
             nc.scalar.activation(out=po[:], in_=pb[:], func=ACT.Tanh)
             nc.sync.dma_start(out=out_1[0, P * c:P * (c + 1), :], in_=po[:])
 
         th = {}
 
-        def theta_tanh(c):
-            th[c] = work.tile([P, CL], F32, name="th_%d" % c, tag="th", bufs=2)
-            src = tbank[c][:].rearrange("p (di dj a j) -> p dj a di j", di=2, dj=2, a=16, j=8)
-            dst = th[c][:].rearrange("p (dj a di j) -> p dj a di j", dj=2, a=16, di=2, j=8)
-            for dj in range(2):
-                nc.scalar.activation(out=dst[:, dj], in_=src[:, dj], func=ACT.Tanh, bias=bth[:, 0:1])
+        def theta_tanh(c, di):
+            if di == 0:
+                th[c] = work.tile([P, CL], F32, name="th_%d" % c, tag="th", bufs=2)
+            src = tbank[c][:].rearrange("p (di dj a j) -> p di dj a j", di=2, dj=2, a=16, j=8)
+            dst = th[c][:].rearrange("p (dj a di j) -> p di dj a j", dj=2, a=16, di=2, j=8)
+            nc.scalar.activation(out=dst[:, di], in_=src[:, di], func=ACT.Tanh, bias=bth[:, 0:1])
 
         out0v = out_0[0].rearrange("(c f p dj) k -> c p f (dj k)", c=NCHUNK, f=2, p=P, dj=2)
 
@@ -245,27 +263,54 @@ def tile_selfattention3d_pb_kernel(
             wquant(g, 256, 768)
         widen(1, 1)
 
-        for c in range(NCHUNK):
-            nxt = c + 1 < NCHUNK
+        for c in range(NCHUNK - 1):
+            last = c + 1 == NCHUNK - 1
             mm_theta(c)
             for w in range(4):
                 mm_tile(c, w)
-            if nxt:
-                inter(c + 1, 0)
-            if c + 2 < NCHUNK:
+            inter(c + 1, 0)
+            if not last:
                 widen(c + 2, 0)
-            theta_tanh(c)
+            theta_tanh(c, 0)
+            theta_tanh(c, 1)
             g_first(c)
             g_max(c, 1)
-            if nxt:
-                quant(c + 1, 0)
+            quant(c + 1, 0)
+            if last:
+                inter_half(c + 1, 1, 0)
+                theta_out(c)
+                g_max(c, 2)
+                quant(c + 1, 1, 0, CL // 2)
+                inter_half(c + 1, 1, 1)
+                g_max(c, 3)
+                quant(c + 1, 1, CL // 2, CL)
+            else:
                 inter(c + 1, 1)
-            theta_out(c)
-            g_max(c, 2)
-            if nxt:
+                theta_out(c)
+                g_max(c, 2)
                 quant(c + 1, 1)
-            g_max(c, 3)
-            if c + 2 < NCHUNK:
+                g_max(c, 3)
                 widen(c + 2, 1)
-            phi_all(c)
+            phi_pool(c)
+            phi_last(c)
             g_last(c)
+
+        c = NCHUNK - 1
+        mm_tile(c, 0)
+        mm_tile(c, 1)
+        mm_theta(c, 0, CL // 2)
+        g_first(c)
+        theta_tanh(c, 0)
+        g_max(c, 1)
+        mm_tile(c, 2)
+        mm_tile(c, 3)
+        mm_theta(c, CL // 2, CL)
+        g_max(c, 2)
+        theta_tanh(c, 1)
+        g_max(c, 3)
+        theta_out(c)
+        phi_pool(c)
+        phi_last(c)
+        for lo in (0, 256):
+            g_bias(c, nc.vector, lo, lo + 256)
+            g_store(c, lo, lo + 256)

@@ -20,7 +20,7 @@ NCHUNK = 4
 NPASS = 2
 CL = 512
 
-V_WIDEN = ((0, 0),)
+V_WIDEN = {(0, 0): 2, (0, 1): 2, (1, 0): 2, (1, 1): 1}
 W_COPY_ON_SCALAR = (True, True, True, True, True, True)
 U_COPY_ON_SCALAR = True
 G_BIAS = (2,)
@@ -87,13 +87,14 @@ def tile_selfattention3d_pb_kernel(
         xc = {}
         xs = {}
 
-        def widen(c, g):
-            wd = work.tile([P, 4, CL], BF16, name="wide_%d_%d" % (c, g), tag="wide", bufs=4)
-            wide[(c, g)] = wd
+        def widen(c, g, planes=(0, 1, 2, 3)):
+            if (c, g) not in wide:
+                wide[(c, g)] = work.tile([P, 4, CL], BF16, name="wide_%d_%d" % (c, g), tag="wide", bufs=4)
+            wd = wide[(c, g)]
             src = xbytes[(c, g)]
-            for t in range(4):
+            for t in planes:
                 col = xsc[:, 4 * g + t:4 * g + t + 1]
-                if (c, g) in V_WIDEN:
+                if t < V_WIDEN.get((c, g), 0):
                     nc.vector.tensor_scalar(
                         out=wd[:, t, :], in0=src[:, t, :].bitcast(FP8), scalar1=col, scalar2=None, op0=ALU.mult
                     )
@@ -213,12 +214,15 @@ def tile_selfattention3d_pb_kernel(
             pooled[c] = work.tile([P, P], F32, name="pr_%d" % c, tag="pr", bufs=2)
             nc.vector.tensor_reduce(out=pooled[c][:], in_=fbank[c][:].rearrange("p w k -> p k w"), axis=AX.X, op=ALU.max)
 
-        def phi_last(c):
-            pr = pooled[c]
-            pb = work.tile([P, P], F32, name="pb_%d" % c, tag="pb", bufs=2)
-            nc.vector.tensor_tensor(out=pb[:], in0=pr[:], in1=bphi[:], op=ALU.add)
+        biased = {}
+
+        def phi_add(c):
+            biased[c] = work.tile([P, P], F32, name="pb_%d" % c, tag="pb", bufs=2)
+            nc.vector.tensor_tensor(out=biased[c][:], in0=pooled[c][:], in1=bphi[:], op=ALU.add)
+
+        def phi_tanh(c):
             po = work.tile([P, P], F32, name="po_%d" % c, tag="po", bufs=2)
-            nc.scalar.activation(out=po[:], in_=pb[:], func=ACT.Tanh)
+            nc.scalar.activation(out=po[:], in_=biased[c][:], func=ACT.Tanh)
             nc.sync.dma_start(out=out_1[0, P * c:P * (c + 1), :], in_=po[:])
 
         th = {}
@@ -245,72 +249,114 @@ def tile_selfattention3d_pb_kernel(
                 nc.vector.tensor_copy(out=to[:], in_=ub[:])
             nc.sync.dma_start(out=out0v[c], in_=to[:].rearrange("p (f dj) k -> p f (dj k)", f=2))
 
+        ctx.enter_context(tc.manual_schedule(engines={mybir.EngineType.DVE, mybir.EngineType.Activation}))
         widen(0, 0)
         widen(0, 1)
         inter(0, 0)
         wprep(0, 0)
         wprep(0, 1)
+        inter_half(0, 1, 0)
         quant(0, 0)
-        inter(0, 1)
+        inter_half(0, 1, 1)
+        widen(1, 0, (0, 2))
         wprep(1, 0)
         wprep(1, 1)
         quant(0, 1)
+        widen(1, 0, (1, 3))
+        wquant(0, 0, 256)
+        wquant(1, 0, 256)
         wprep(2, 0)
         wprep(2, 1)
-        widen(1, 0)
-        for g in range(NPASS):
-            wquant(g, 0, 256)
-            wquant(g, 256, 768)
+        inter_half(1, 0, 0)
         widen(1, 1)
+        wquant(0, 256, 768)
+        wquant(1, 256, 768)
+        inter_half(1, 0, 1)
+        widen(2, 0)
+        mm_theta(0)
+        for w in range(4):
+            mm_tile(0, w)
+        inter_half(1, 1, 0)
+        quant(1, 0)
+        inter_half(1, 1, 1)
+        phi_pool(0)
+        quant(1, 1)
 
-        for c in range(NCHUNK - 1):
-            last = c + 1 == NCHUNK - 1
-            mm_theta(c)
-            for w in range(4):
-                mm_tile(c, w)
-            inter(c + 1, 0)
-            if not last:
-                widen(c + 2, 0)
-            theta_tanh(c, 0)
-            theta_tanh(c, 1)
-            g_first(c)
-            g_max(c, 1)
-            quant(c + 1, 0)
-            if last:
-                inter_half(c + 1, 1, 0)
-                theta_out(c)
-                g_max(c, 2)
-                quant(c + 1, 1, 0, CL // 2)
-                inter_half(c + 1, 1, 1)
-                g_max(c, 3)
-                quant(c + 1, 1, CL // 2, CL)
-            else:
-                inter(c + 1, 1)
-                theta_out(c)
-                g_max(c, 2)
-                quant(c + 1, 1)
-                g_max(c, 3)
-                widen(c + 2, 1)
-            phi_pool(c)
-            phi_last(c)
-            g_last(c)
+        theta_tanh(0, 0)
+        theta_tanh(0, 1)
+        g_first(0)
+        widen(2, 1, (0,))
+        theta_out(0)
+        widen(2, 1, (1, 2, 3))
+        phi_add(0)
+        phi_tanh(0)
+        widen(3, 0)
+        mm_theta(1)
+        inter_half(2, 0, 0)
+        g_max(0, 1)
+        inter_half(2, 0, 1)
+        g_max(0, 2)
+        quant(2, 0)
+        g_max(0, 3)
+        for w in range(4):
+            mm_tile(1, w)
+        inter_half(2, 1, 0)
+        g_last(0)
+        inter_half(2, 1, 1)
+        phi_pool(1)
+        quant(2, 1)
 
-        c = NCHUNK - 1
-        mm_tile(c, 0)
-        mm_tile(c, 1)
-        mm_theta(c, 0, CL // 2)
-        g_first(c)
-        theta_tanh(c, 0)
-        g_max(c, 1)
-        mm_tile(c, 2)
-        mm_tile(c, 3)
-        mm_theta(c, CL // 2, CL)
-        g_max(c, 2)
-        theta_tanh(c, 1)
-        g_max(c, 3)
-        theta_out(c)
-        phi_pool(c)
-        phi_last(c)
+        theta_tanh(1, 0)
+        theta_tanh(1, 1)
+        g_first(1)
+        widen(3, 1, (0,))
+        theta_out(1)
+        widen(3, 1, (1, 2, 3))
+        phi_add(1)
+        phi_tanh(1)
+        mm_theta(2)
+        g_max(1, 1)
+        inter_half(3, 0, 0)
+        g_max(1, 2)
+        inter_half(3, 0, 1)
+        g_max(1, 3)
+        for w in range(4):
+            mm_tile(2, w)
+        quant(3, 0)
+        g_last(1)
+
+        theta_tanh(2, 0)
+        theta_tanh(2, 1)
+        g_first(2)
+        theta_out(2)
+        g_max(2, 1)
+        inter_half(3, 1, 0)
+        g_max(2, 2)
+        quant(3, 1, 0, CL // 2)
+        phi_pool(2)
+        inter_half(3, 1, 1)
+        mm_tile(3, 0)
+        mm_tile(3, 1)
+        mm_theta(3, 0, CL // 2)
+        g_max(2, 3)
+        quant(3, 1, CL // 2, CL)
+        g_last(2)
+
+        g_first(3)
+        g_max(3, 1)
+        theta_tanh(3, 0)
+        phi_add(2)
+        mm_tile(3, 2)
+        mm_theta(3, CL // 2, CL)
+        mm_tile(3, 3)
+        g_max(3, 2)
+        phi_pool(3)
+        theta_tanh(3, 1)
+        phi_tanh(2)
+        theta_out(3)
+        g_max(3, 3)
+        phi_add(3)
+        phi_tanh(3)
         for lo in (0, 256):
-            g_bias(c, nc.vector, lo, lo + 256)
-            g_store(c, lo, lo + 256)
+            g_bias(3, nc.vector, lo, lo + 256)
+            g_store(3, lo, lo + 256)

@@ -20,7 +20,8 @@ NCHUNK = 4
 NPASS = 2
 CL = 512
 
-V_WIDEN = {(0, 0): 2, (0, 1): 2, (1, 0): 2, (1, 1): 1}
+V_WIDEN = {(0, 0): 4, (1, 0): 1}
+PAIRED = (0, 0)
 W_COPY_ON_SCALAR = (True, True, True, True, True, True)
 U_COPY_ON_SCALAR = True
 G_BIAS = (2,)
@@ -43,18 +44,20 @@ def tile_selfattention3d_pb_kernel(
         xb = x_bytes[0].rearrange("(g p t) f i j -> g p t (f i j)", g=NPASS, p=P, t=4)
         xbytes = {}
 
-        def load_x(c, g):
-            tl = keep.tile([P, 4, CL], U8, name="xbytes_%d_%d" % (c, g), tag="xbytes_%d_%d" % (c, g))
-            nc.sync.dma_start(out=tl[:], in_=xb[g][:, :, c * CL:(c + 1) * CL])
-            xbytes[(c, g)] = tl
+        def load_x(c, g, lo=0, hi=4):
+            if (c, g) not in xbytes:
+                xbytes[(c, g)] = keep.tile([P, 4, CL], U8, name="xbytes_%d_%d" % (c, g), tag="xbytes_%d_%d" % (c, g))
+            nc.sync.dma_start(out=xbytes[(c, g)][:, lo:hi, :], in_=xb[g][:, lo:hi, c * CL:(c + 1) * CL])
 
         wraw = []
         for r in range(6):
             wraw.append(keep.tile([P, 1024], BF16, name="wraw%d" % r, tag="wraw%d" % r))
         wg_rows = w_g.rearrange("(r p) k -> r p k", p=P)
 
-        load_x(0, 0)
-        load_x(0, 1)
+        load_x(0, 0, 0, 2)
+        load_x(0, 1, 0, 2)
+        load_x(0, 0, 2, 4)
+        load_x(0, 1, 2, 4)
         nc.sync.dma_start(out=wraw[0][:], in_=w_theta)
         nc.sync.dma_start(out=wraw[1][:], in_=w_phi)
         load_x(1, 0)
@@ -89,25 +92,34 @@ def tile_selfattention3d_pb_kernel(
 
         def widen(c, g, planes=(0, 1, 2, 3)):
             if (c, g) not in wide:
-                wide[(c, g)] = work.tile([P, 4, CL], BF16, name="wide_%d_%d" % (c, g), tag="wide", bufs=4)
+                shape = [P, 2, CL, 2] if (c, g) == PAIRED else [P, 4, CL]
+                wide[(c, g)] = work.tile(shape, BF16, name="wide_%d_%d" % (c, g), tag="wide", bufs=4)
             wd = wide[(c, g)]
             src = xbytes[(c, g)]
             for t in planes:
                 col = xsc[:, 4 * g + t:4 * g + t + 1]
                 if t < V_WIDEN.get((c, g), 0):
                     nc.vector.tensor_scalar(
-                        out=wd[:, t, :], in0=src[:, t, :].bitcast(FP8), scalar1=col, scalar2=None, op0=ALU.mult
+                        out=wd[:, t // 2, :, t % 2] if (c, g) == PAIRED else wd[:, t, :],
+                        in0=src[:, t, :].bitcast(FP8), scalar1=col, scalar2=None, op0=ALU.mult
                     )
                 else:
                     nc.scalar.activation(out=wd[:, t, :], in_=src[:, t, :].bitcast(FP8), func=ACT.Copy, scale=col)
 
-        def inter_half(c, g, di):
+        def inter_half(c, g, di, on_scalar=False):
             if di == 0:
                 grp[(c, g)] = work.tile([P, CL, 4], BF16, name="grp_%d_%d" % (c, g), tag="grp", bufs=3, align_bytes=64)
             gr = grp[(c, g)]
-            src = wide[(c, g)][:].rearrange("p t (a di j b dj) -> p di a j t b dj", a=16, di=2, j=4, b=2, dj=2)
-            dst = gr[:].rearrange("p (di dj a j b) t -> p di a j t b dj", di=2, dj=2, a=16, j=4, b=2)
-            nc.vector.tensor_copy(out=dst[:, di], in_=src[:, di])
+            if (c, g) == PAIRED:
+                src = wide[(c, g)][:].rearrange("p h (a di j dj) l -> p di a j dj h l", a=16, di=2, j=8, dj=2)
+                dst = gr[:].rearrange("p (di dj a j) (h l) -> p di a j dj h l", di=2, dj=2, a=16, j=8, h=2)
+            else:
+                src = wide[(c, g)][:].rearrange("p t (a di j b dj) -> p di a j t b dj", a=16, di=2, j=4, b=2, dj=2)
+                dst = gr[:].rearrange("p (di dj a j b) t -> p di a j t b dj", di=2, dj=2, a=16, j=4, b=2)
+            if on_scalar:
+                nc.scalar.copy(out=dst[:, di], in_=src[:, di])
+            else:
+                nc.vector.tensor_copy(out=dst[:, di], in_=src[:, di])
 
         def inter(c, g):
             for di in range(2):
@@ -154,36 +166,45 @@ def tile_selfattention3d_pb_kernel(
         fbank = {}
         gbank = {}
 
-        def mm_theta(c, lo=0, hi=CL):
-            if lo == 0:
+        def mm_theta(c, g, lo=0, hi=CL):
+            if lo == 0 and g == 0:
                 tbank[c] = psum.tile([P, CL], F32, name="T_%d" % c, tag="T", bufs=1)
-            for g in range(NPASS):
-                nc.tensor.matmul_mx(
-                    out=tbank[c][:, lo:hi],
-                    lhsT=wc[g][:, 0:128].bitcast(FP8X4), lhsT_scale=wsc[g][:, 0:128],
-                    rhs=xc[(c, g)][:, lo:hi].bitcast(FP8X4), rhs_scale=xs[(c, g)][:, lo:hi],
-                    start=(g == 0), stop=(g == NPASS - 1),
-                )
+            nc.tensor.matmul_mx(
+                out=tbank[c][:, lo:hi],
+                lhsT=wc[g][:, 0:128].bitcast(FP8X4), lhsT_scale=wsc[g][:, 0:128],
+                rhs=xc[(c, g)][:, lo:hi].bitcast(FP8X4), rhs_scale=xs[(c, g)][:, lo:hi],
+                start=(g == 0), stop=(g == NPASS - 1),
+            )
 
-        def mm_tile(c, w):
-            if w == 0:
-                fbank[c] = psum.tile([P, 4, P], F32, name="F_%d" % c, tag="F", bufs=1)
-            gb = psum.tile([P, 512], F32, name="G_%d_%d" % (c, w), tag="G", bufs=5)
-            gbank[(c, w)] = gb
+        def mm_g(c, w, g):
+            if g == 0:
+                gbank[(c, w)] = psum.tile([P, 512], F32, name="G_%d_%d" % (c, w), tag="G", bufs=5)
             cols = slice(P * w, P * (w + 1))
+            nc.tensor.matmul_mx(
+                out=gbank[(c, w)][:],
+                lhsT=xc[(c, g)][:, cols].bitcast(FP8X4), lhsT_scale=xs[(c, g)][:, cols],
+                rhs=wc[g][:, 256:768].bitcast(FP8X4), rhs_scale=wsc[g][:, 256:768],
+                start=(g == 0), stop=(g == NPASS - 1),
+            )
+
+        def mm_phi(c, w, g):
+            if w == 0 and g == 0:
+                fbank[c] = psum.tile([P, 4, P], F32, name="F_%d" % c, tag="F", bufs=1)
+            cols = slice(P * w, P * (w + 1))
+            nc.tensor.matmul_mx(
+                out=fbank[c][:, w, :],
+                lhsT=xc[(c, g)][:, cols].bitcast(FP8X4), lhsT_scale=xs[(c, g)][:, cols],
+                rhs=wc[g][:, 128:256].bitcast(FP8X4), rhs_scale=wsc[g][:, 128:256],
+                start=(g == 0), stop=(g == NPASS - 1),
+            )
+
+        def mm_chunk(c):
             for g in range(NPASS):
-                lhsT = xc[(c, g)][:, cols].bitcast(FP8X4)
-                lsc = xs[(c, g)][:, cols]
-                nc.tensor.matmul_mx(
-                    out=gb[:], lhsT=lhsT, lhsT_scale=lsc,
-                    rhs=wc[g][:, 256:768].bitcast(FP8X4), rhs_scale=wsc[g][:, 256:768],
-                    start=(g == 0), stop=(g == NPASS - 1),
-                )
-                nc.tensor.matmul_mx(
-                    out=fbank[c][:, w, :], lhsT=lhsT, lhsT_scale=lsc,
-                    rhs=wc[g][:, 128:256].bitcast(FP8X4), rhs_scale=wsc[g][:, 128:256],
-                    start=(g == 0), stop=(g == NPASS - 1),
-                )
+                mm_theta(c, g)
+            for w in range(4):
+                for g in range(NPASS):
+                    mm_g(c, w, g)
+                    mm_phi(c, w, g)
 
         acc = {}
 
@@ -258,11 +279,11 @@ def tile_selfattention3d_pb_kernel(
         inter_half(0, 1, 0)
         quant(0, 0)
         inter_half(0, 1, 1)
-        widen(1, 0, (0, 2))
+        widen(1, 0, (0, 1, 2))
         wprep(1, 0)
         wprep(1, 1)
         quant(0, 1)
-        widen(1, 0, (1, 3))
+        widen(1, 0, (3,))
         wquant(0, 0, 256)
         wquant(1, 0, 256)
         wprep(2, 0)
@@ -273,87 +294,93 @@ def tile_selfattention3d_pb_kernel(
         wquant(1, 256, 768)
         inter_half(1, 0, 1)
         widen(2, 0)
-        mm_theta(0)
-        for w in range(4):
-            mm_tile(0, w)
-        inter_half(1, 1, 0)
+        mm_chunk(0)
         quant(1, 0)
+        inter_half(1, 1, 0)
         inter_half(1, 1, 1)
         phi_pool(0)
         quant(1, 1)
 
+        g_first(0)
         theta_tanh(0, 0)
         theta_tanh(0, 1)
-        g_first(0)
-        widen(2, 1, (0,))
+        widen(2, 1, (0, 1, 2))
         theta_out(0)
-        widen(2, 1, (1, 2, 3))
+        widen(2, 1, (3,))
         phi_add(0)
         phi_tanh(0)
         widen(3, 0)
-        mm_theta(1)
         inter_half(2, 0, 0)
         g_max(0, 1)
         inter_half(2, 0, 1)
         g_max(0, 2)
         quant(2, 0)
         g_max(0, 3)
-        for w in range(4):
-            mm_tile(1, w)
+        mm_chunk(1)
         inter_half(2, 1, 0)
         g_last(0)
         inter_half(2, 1, 1)
         phi_pool(1)
-        quant(2, 1)
 
+        g_first(1)
         theta_tanh(1, 0)
         theta_tanh(1, 1)
-        g_first(1)
-        widen(3, 1, (0,))
+        widen(3, 1, (0, 1, 2))
         theta_out(1)
-        widen(3, 1, (1, 2, 3))
+        widen(3, 1, (3,))
+        quant(2, 1)
         phi_add(1)
         phi_tanh(1)
-        mm_theta(2)
-        g_max(1, 1)
         inter_half(3, 0, 0)
-        g_max(1, 2)
+        g_max(1, 1)
         inter_half(3, 0, 1)
-        g_max(1, 3)
-        for w in range(4):
-            mm_tile(2, w)
+        g_max(1, 2)
+        mm_chunk(2)
         quant(3, 0)
-        g_last(1)
-
+        g_max(1, 3)
+        g_first(2)
         theta_tanh(2, 0)
         theta_tanh(2, 1)
-        g_first(2)
-        theta_out(2)
-        g_max(2, 1)
         inter_half(3, 1, 0)
-        g_max(2, 2)
-        quant(3, 1, 0, CL // 2)
+        inter_half(3, 1, 1, on_scalar=True)
+        mm_g(3, 0, 0)
+        mm_g(3, 1, 0)
+        theta_out(2)
+        mm_theta(3, 0, 0, CL // 2)
+        g_last(1)
+
         phi_pool(2)
-        inter_half(3, 1, 1)
-        mm_tile(3, 0)
-        mm_tile(3, 1)
-        mm_theta(3, 0, CL // 2)
-        g_max(2, 3)
+        g_max(2, 1)
+        mm_g(3, 2, 0)
+        quant(3, 1, 0, CL // 2)
+        mm_g(3, 0, 1)
+        mm_g(3, 1, 1)
+        mm_theta(3, 1, 0, CL // 2)
+        g_max(2, 2)
+        mm_g(3, 3, 0)
+        for w in range(2):
+            for g in range(NPASS):
+                mm_phi(3, w, g)
         quant(3, 1, CL // 2, CL)
+        mm_g(3, 2, 1)
+        g_max(2, 3)
         g_last(2)
 
         g_first(3)
-        g_max(3, 1)
         theta_tanh(3, 0)
+        g_max(3, 1)
         phi_add(2)
-        mm_tile(3, 2)
-        mm_theta(3, CL // 2, CL)
-        mm_tile(3, 3)
+        for g in range(NPASS):
+            mm_theta(3, g, CL // 2, CL)
+        mm_g(3, 3, 1)
+        for w in range(2, 4):
+            for g in range(NPASS):
+                mm_phi(3, w, g)
         g_max(3, 2)
-        phi_pool(3)
         theta_tanh(3, 1)
         phi_tanh(2)
         theta_out(3)
+        phi_pool(3)
         g_max(3, 3)
         phi_add(3)
         phi_tanh(3)

@@ -20,11 +20,10 @@ NCHUNK = 4
 NPASS = 2
 CL = 512
 
-V_WIDEN = {(0, 0): 4, (1, 0): 1}
-PAIRED = (0, 0)
+V_WIDEN = {(0, 0): 2, (0, 1): 2, (1, 0): 1}
 W_COPY_ON_SCALAR = (True, True, True, True, True, True)
 U_COPY_ON_SCALAR = True
-G_BIAS = (2,)
+G_BIAS = (1, 2)
 
 
 def tile_selfattention3d_pb_kernel(
@@ -54,10 +53,9 @@ def tile_selfattention3d_pb_kernel(
             wraw.append(keep.tile([P, 1024], BF16, name="wraw%d" % r, tag="wraw%d" % r))
         wg_rows = w_g.rearrange("(r p) k -> r p k", p=P)
 
-        load_x(0, 0, 0, 2)
-        load_x(0, 1, 0, 2)
-        load_x(0, 0, 2, 4)
-        load_x(0, 1, 2, 4)
+        for g in range(NPASS):
+            for lo in (0, 2):
+                load_x(0, g, lo, lo + 2)
         nc.sync.dma_start(out=wraw[0][:], in_=w_theta)
         nc.sync.dma_start(out=wraw[1][:], in_=w_phi)
         load_x(1, 0)
@@ -92,16 +90,14 @@ def tile_selfattention3d_pb_kernel(
 
         def widen(c, g, planes=(0, 1, 2, 3)):
             if (c, g) not in wide:
-                shape = [P, 2, CL, 2] if (c, g) == PAIRED else [P, 4, CL]
-                wide[(c, g)] = work.tile(shape, BF16, name="wide_%d_%d" % (c, g), tag="wide", bufs=4)
+                wide[(c, g)] = work.tile([P, 4, CL], BF16, name="wide_%d_%d" % (c, g), tag="wide", bufs=4)
             wd = wide[(c, g)]
             src = xbytes[(c, g)]
             for t in planes:
                 col = xsc[:, 4 * g + t:4 * g + t + 1]
                 if t < V_WIDEN.get((c, g), 0):
                     nc.vector.tensor_scalar(
-                        out=wd[:, t // 2, :, t % 2] if (c, g) == PAIRED else wd[:, t, :],
-                        in0=src[:, t, :].bitcast(FP8), scalar1=col, scalar2=None, op0=ALU.mult
+                        out=wd[:, t, :], in0=src[:, t, :].bitcast(FP8), scalar1=col, scalar2=None, op0=ALU.mult
                     )
                 else:
                     nc.scalar.activation(out=wd[:, t, :], in_=src[:, t, :].bitcast(FP8), func=ACT.Copy, scale=col)
@@ -110,12 +106,8 @@ def tile_selfattention3d_pb_kernel(
             if di == 0:
                 grp[(c, g)] = work.tile([P, CL, 4], BF16, name="grp_%d_%d" % (c, g), tag="grp", bufs=3, align_bytes=64)
             gr = grp[(c, g)]
-            if (c, g) == PAIRED:
-                src = wide[(c, g)][:].rearrange("p h (a di j dj) l -> p di a j dj h l", a=16, di=2, j=8, dj=2)
-                dst = gr[:].rearrange("p (di dj a j) (h l) -> p di a j dj h l", di=2, dj=2, a=16, j=8, h=2)
-            else:
-                src = wide[(c, g)][:].rearrange("p t (a di j b dj) -> p di a j t b dj", a=16, di=2, j=4, b=2, dj=2)
-                dst = gr[:].rearrange("p (di dj a j b) t -> p di a j t b dj", di=2, dj=2, a=16, j=4, b=2)
+            src = wide[(c, g)][:].rearrange("p t (a di j b dj) -> p di a j t b dj", a=16, di=2, j=4, b=2, dj=2)
+            dst = gr[:].rearrange("p (di dj a j b) t -> p di a j t b dj", di=2, dj=2, a=16, j=4, b=2)
             if on_scalar:
                 nc.scalar.copy(out=dst[:, di], in_=src[:, di])
             else:
@@ -198,13 +190,10 @@ def tile_selfattention3d_pb_kernel(
                 start=(g == 0), stop=(g == NPASS - 1),
             )
 
-        def mm_chunk(c):
+        def mm_window(c, w):
             for g in range(NPASS):
-                mm_theta(c, g)
-            for w in range(4):
-                for g in range(NPASS):
-                    mm_g(c, w, g)
-                    mm_phi(c, w, g)
+                mm_g(c, w, g)
+                mm_phi(c, w, g)
 
         acc = {}
 
@@ -270,7 +259,7 @@ def tile_selfattention3d_pb_kernel(
                 nc.vector.tensor_copy(out=to[:], in_=ub[:])
             nc.sync.dma_start(out=out0v[c], in_=to[:].rearrange("p (f dj) k -> p f (dj k)", f=2))
 
-        ctx.enter_context(tc.manual_schedule(engines={mybir.EngineType.DVE, mybir.EngineType.Activation}))
+        ctx.enter_context(tc.manual_schedule(engines={mybir.EngineType.DVE, mybir.EngineType.Activation, mybir.EngineType.PE}))
         widen(0, 0)
         widen(0, 1)
         inter(0, 0)
@@ -294,7 +283,10 @@ def tile_selfattention3d_pb_kernel(
         wquant(1, 256, 768)
         inter_half(1, 0, 1)
         widen(2, 0)
-        mm_chunk(0)
+        mm_theta(0, 0)
+        mm_theta(0, 1)
+        for w in range(4):
+            mm_window(0, w)
         quant(1, 0)
         inter_half(1, 1, 0)
         inter_half(1, 1, 1)
@@ -304,19 +296,23 @@ def tile_selfattention3d_pb_kernel(
         g_first(0)
         theta_tanh(0, 0)
         theta_tanh(0, 1)
-        widen(2, 1, (0, 1, 2))
-        theta_out(0)
-        widen(2, 1, (3,))
+        widen(2, 1)
+        mm_window(1, 0)
+        mm_window(1, 1)
         phi_add(0)
         phi_tanh(0)
+        theta_out(0)
         widen(3, 0)
+        mm_theta(1, 0)
+        mm_theta(1, 1)
         inter_half(2, 0, 0)
         g_max(0, 1)
         inter_half(2, 0, 1)
         g_max(0, 2)
         quant(2, 0)
         g_max(0, 3)
-        mm_chunk(1)
+        mm_window(1, 2)
+        mm_window(1, 3)
         inter_half(2, 1, 0)
         g_last(0)
         inter_half(2, 1, 1)
@@ -325,62 +321,65 @@ def tile_selfattention3d_pb_kernel(
         g_first(1)
         theta_tanh(1, 0)
         theta_tanh(1, 1)
-        widen(3, 1, (0, 1, 2))
-        theta_out(1)
-        widen(3, 1, (3,))
+        widen(3, 1)
         quant(2, 1)
+        mm_window(2, 0)
+        mm_window(2, 1)
+        theta_out(1)
         phi_add(1)
         phi_tanh(1)
         inter_half(3, 0, 0)
+        mm_theta(2, 0)
+        mm_theta(2, 1)
         g_max(1, 1)
         inter_half(3, 0, 1)
         g_max(1, 2)
-        mm_chunk(2)
+        mm_window(2, 2)
+        mm_window(2, 3)
         quant(3, 0)
-        g_max(1, 3)
         g_first(2)
         theta_tanh(2, 0)
         theta_tanh(2, 1)
         inter_half(3, 1, 0)
         inter_half(3, 1, 1, on_scalar=True)
+        g_max(1, 3)
         mm_g(3, 0, 0)
         mm_g(3, 1, 0)
-        theta_out(2)
-        mm_theta(3, 0, 0, CL // 2)
-        g_last(1)
-
-        phi_pool(2)
-        g_max(2, 1)
-        mm_g(3, 2, 0)
         quant(3, 1, 0, CL // 2)
+        g_last(1)
         mm_g(3, 0, 1)
         mm_g(3, 1, 1)
-        mm_theta(3, 1, 0, CL // 2)
-        g_max(2, 2)
-        mm_g(3, 3, 0)
+
+        phi_pool(2)
+        for g in range(NPASS):
+            mm_theta(3, g, 0, CL // 2)
         for w in range(2):
             for g in range(NPASS):
                 mm_phi(3, w, g)
-        quant(3, 1, CL // 2, CL)
-        mm_g(3, 2, 1)
-        g_max(2, 3)
-        g_last(2)
-
+        g_max(2, 1)
+        phi_add(2)
         g_first(3)
         theta_tanh(3, 0)
-        g_max(3, 1)
-        phi_add(2)
+        theta_out(2)
+        mm_g(3, 2, 0)
+        quant(3, 1, CL // 2, CL)
+        mm_g(3, 2, 1)
         for g in range(NPASS):
             mm_theta(3, g, CL // 2, CL)
+        g_max(2, 2)
+        mm_g(3, 3, 0)
         mm_g(3, 3, 1)
+        g_max(3, 1)
+        g_max(2, 3)
+        g_last(2)
         for w in range(2, 4):
             for g in range(NPASS):
                 mm_phi(3, w, g)
-        g_max(3, 2)
         theta_tanh(3, 1)
+        g_max(3, 2)
+        phi_pool(3)
         phi_tanh(2)
         theta_out(3)
-        phi_pool(3)
         g_max(3, 3)
         phi_add(3)
         phi_tanh(3)

@@ -23,7 +23,7 @@ CL = 512
 V_WIDEN = {(0, 0): 2, (0, 1): 2, (1, 0): 1}
 W_COPY_ON_SCALAR = (True, True, True, True, True, True)
 U_COPY_ON_SCALAR = True
-G_BIAS = (1, 2)
+G_BIAS = (2,)
 
 
 def tile_selfattention3d_pb_kernel(

@@ -20,9 +20,8 @@ NCHUNK = 4
 NPASS = 2
 CL = 512
 
-V_WIDEN = {(0, 0): 2, (0, 1): 2, (1, 0): 1}
+V_WIDEN = {(0, 0): 2, (0, 1): 1, (1, 0): 1}
 W_COPY_ON_SCALAR = (True, True, True, True, True, True)
-U_COPY_ON_SCALAR = True
 G_BIAS = (2,)
 
 
@@ -43,19 +42,17 @@ def tile_selfattention3d_pb_kernel(
         xb = x_bytes[0].rearrange("(g p t) f i j -> g p t (f i j)", g=NPASS, p=P, t=4)
         xbytes = {}
 
-        def load_x(c, g, lo=0, hi=4):
-            if (c, g) not in xbytes:
-                xbytes[(c, g)] = keep.tile([P, 4, CL], U8, name="xbytes_%d_%d" % (c, g), tag="xbytes_%d_%d" % (c, g))
-            nc.sync.dma_start(out=xbytes[(c, g)][:, lo:hi, :], in_=xb[g][:, lo:hi, c * CL:(c + 1) * CL])
+        def load_x(c, g):
+            xbytes[(c, g)] = keep.tile([P, 4, CL], U8, name="xbytes_%d_%d" % (c, g), tag="xbytes_%d_%d" % (c, g))
+            nc.sync.dma_start(out=xbytes[(c, g)][:], in_=xb[g][:, :, c * CL:(c + 1) * CL])
 
         wraw = []
         for r in range(6):
             wraw.append(keep.tile([P, 1024], BF16, name="wraw%d" % r, tag="wraw%d" % r))
         wg_rows = w_g.rearrange("(r p) k -> r p k", p=P)
 
-        for g in range(NPASS):
-            for lo in (0, 2):
-                load_x(0, g, lo, lo + 2)
+        load_x(0, 0)
+        load_x(0, 1)
         nc.sync.dma_start(out=wraw[0][:], in_=w_theta)
         nc.sync.dma_start(out=wraw[1][:], in_=w_phi)
         load_x(1, 0)
@@ -66,8 +63,8 @@ def tile_selfattention3d_pb_kernel(
         nc.sync.dma_start(out=wraw[5][:], in_=wg_rows[3])
         bth = keep.tile([P, 1], BF16, name="bth", tag="bth")
         nc.sync.dma_start(out=bth[:], in_=b_theta.rearrange("(p o) -> p o", o=1))
-        bphi = keep.tile([P, 128], BF16, name="bphi", tag="bphi")
-        nc.sync.dma_start(out=bphi[:], in_=b_phi.partition_broadcast(P))
+        bphi = keep.tile([P, 1], BF16, name="bphi", tag="bphi")
+        nc.sync.dma_start(out=bphi[:], in_=b_phi.rearrange("(p o) -> p o", o=1))
         bg = keep.tile([P, 512], BF16, name="bg", tag="bg")
         nc.sync.dma_start(out=bg[:], in_=b_g.partition_broadcast(P))
         for c in range(2, NCHUNK):
@@ -179,21 +176,19 @@ def tile_selfattention3d_pb_kernel(
                 start=(g == 0), stop=(g == NPASS - 1),
             )
 
-        def mm_phi(c, w, g):
-            if w == 0 and g == 0:
-                fbank[c] = psum.tile([P, 4, P], F32, name="F_%d" % c, tag="F", bufs=1)
-            cols = slice(P * w, P * (w + 1))
-            nc.tensor.matmul_mx(
-                out=fbank[c][:, w, :],
-                lhsT=xc[(c, g)][:, cols].bitcast(FP8X4), lhsT_scale=xs[(c, g)][:, cols],
-                rhs=wc[g][:, 128:256].bitcast(FP8X4), rhs_scale=wsc[g][:, 128:256],
-                start=(g == 0), stop=(g == NPASS - 1),
-            )
+        def mm_phi(c):
+            fbank[c] = psum.tile([P, CL], F32, name="F_%d" % c, tag="F", bufs=1)
+            for g in range(NPASS):
+                nc.tensor.matmul_mx(
+                    out=fbank[c][:],
+                    lhsT=wc[g][:, 128:256].bitcast(FP8X4), lhsT_scale=wsc[g][:, 128:256],
+                    rhs=xc[(c, g)][:].bitcast(FP8X4), rhs_scale=xs[(c, g)][:],
+                    start=(g == 0), stop=(g == NPASS - 1),
+                )
 
         def mm_window(c, w):
             for g in range(NPASS):
                 mm_g(c, w, g)
-                mm_phi(c, w, g)
 
         acc = {}
 
@@ -222,17 +217,25 @@ def tile_selfattention3d_pb_kernel(
 
         def phi_pool(c):
             pooled[c] = work.tile([P, P], F32, name="pr_%d" % c, tag="pr", bufs=2)
-            nc.vector.tensor_reduce(out=pooled[c][:], in_=fbank[c][:].rearrange("p w k -> p k w"), axis=AX.X, op=ALU.max)
+            nc.vector.tensor_reduce(
+                out=pooled[c][:], in_=fbank[c][:].rearrange("p (w m) -> p m w", w=4), axis=AX.X, op=ALU.max
+            )
 
-        biased = {}
-
-        def phi_add(c):
-            biased[c] = work.tile([P, P], F32, name="pb_%d" % c, tag="pb", bufs=2)
-            nc.vector.tensor_tensor(out=biased[c][:], in0=pooled[c][:], in1=bphi[:], op=ALU.add)
+        ph = {}
 
         def phi_tanh(c):
+            ph[c] = work.tile([P, P], F32, name="ph_%d" % c, tag="ph", bufs=2)
+            nc.scalar.activation(out=ph[c][:], in_=pooled[c][:], func=ACT.Tanh, bias=bphi[:, 0:1])
+
+        turned = {}
+
+        def phi_turn(c):
+            turned[c] = psum.tile([P, P], F32, name="FT_%d" % c, tag="F", bufs=1)
+            nc.tensor.transpose(turned[c][:], ph[c][:], ident[:])
+
+        def phi_out(c):
             po = work.tile([P, P], F32, name="po_%d" % c, tag="po", bufs=2)
-            nc.scalar.activation(out=po[:], in_=biased[c][:], func=ACT.Tanh)
+            nc.scalar.copy(out=po[:], in_=turned[c][:])
             nc.sync.dma_start(out=out_1[0, P * c:P * (c + 1), :], in_=po[:])
 
         th = {}
@@ -246,17 +249,18 @@ def tile_selfattention3d_pb_kernel(
 
         out0v = out_0[0].rearrange("(c f p dj) k -> c p f (dj k)", c=NCHUNK, f=2, p=P, dj=2)
 
-        def theta_out(c):
-            ub = psum.tile([P, 4, P], F32, name="U_%d" % c, tag="U", bufs=1)
+        ubank = {}
+
+        def theta_turn(c):
+            ubank[c] = psum.tile([P, 4, P], F32, name="U_%d" % c, tag="U", bufs=1)
             for dj in range(2):
                 for f in range(2):
                     b = 2 * dj + f
-                    nc.tensor.transpose(ub[:, 2 * f + dj, :], th[c][:, P * b:P * (b + 1)], ident[:])
+                    nc.tensor.transpose(ubank[c][:, 2 * f + dj, :], th[c][:, P * b:P * (b + 1)], ident[:])
+
+        def theta_out(c):
             to = work.tile([P, 4, P], F32, name="tho_%d" % c, tag="tho", bufs=2)
-            if U_COPY_ON_SCALAR:
-                nc.scalar.copy(out=to[:], in_=ub[:])
-            else:
-                nc.vector.tensor_copy(out=to[:], in_=ub[:])
+            nc.scalar.copy(out=to[:], in_=ubank[c][:])
             nc.sync.dma_start(out=out0v[c], in_=to[:].rearrange("p (f dj) k -> p f (dj k)", f=2))
 
         ctx.enter_context(tc.manual_schedule(engines={mybir.EngineType.DVE, mybir.EngineType.Activation, mybir.EngineType.PE}))
@@ -283,10 +287,11 @@ def tile_selfattention3d_pb_kernel(
         wquant(1, 256, 768)
         inter_half(1, 0, 1)
         widen(2, 0)
-        mm_theta(0, 0)
-        mm_theta(0, 1)
+        for g in range(NPASS):
+            mm_theta(0, g)
         for w in range(4):
             mm_window(0, w)
+        mm_phi(0)
         quant(1, 0)
         inter_half(1, 1, 0)
         inter_half(1, 1, 1)
@@ -296,15 +301,17 @@ def tile_selfattention3d_pb_kernel(
         g_first(0)
         theta_tanh(0, 0)
         theta_tanh(0, 1)
-        widen(2, 1)
+        phi_tanh(0)
         mm_window(1, 0)
         mm_window(1, 1)
-        phi_add(0)
-        phi_tanh(0)
+        theta_turn(0)
+        phi_turn(0)
+        for g in range(NPASS):
+            mm_theta(1, g)
+        widen(2, 1)
         theta_out(0)
+        phi_out(0)
         widen(3, 0)
-        mm_theta(1, 0)
-        mm_theta(1, 1)
         inter_half(2, 0, 0)
         g_max(0, 1)
         inter_half(2, 0, 1)
@@ -313,6 +320,7 @@ def tile_selfattention3d_pb_kernel(
         g_max(0, 3)
         mm_window(1, 2)
         mm_window(1, 3)
+        mm_phi(1)
         inter_half(2, 1, 0)
         g_last(0)
         inter_half(2, 1, 1)
@@ -321,21 +329,24 @@ def tile_selfattention3d_pb_kernel(
         g_first(1)
         theta_tanh(1, 0)
         theta_tanh(1, 1)
-        widen(3, 1)
+        phi_tanh(1)
         quant(2, 1)
         mm_window(2, 0)
         mm_window(2, 1)
+        theta_turn(1)
+        phi_turn(1)
+        widen(3, 1)
         theta_out(1)
-        phi_add(1)
-        phi_tanh(1)
+        phi_out(1)
         inter_half(3, 0, 0)
-        mm_theta(2, 0)
-        mm_theta(2, 1)
+        for g in range(NPASS):
+            mm_theta(2, g)
         g_max(1, 1)
         inter_half(3, 0, 1)
         g_max(1, 2)
         mm_window(2, 2)
         mm_window(2, 3)
+        mm_phi(2)
         quant(3, 0)
         g_first(2)
         theta_tanh(2, 0)
@@ -351,16 +362,16 @@ def tile_selfattention3d_pb_kernel(
         mm_g(3, 1, 1)
 
         phi_pool(2)
+        phi_tanh(2)
         for g in range(NPASS):
             mm_theta(3, g, 0, CL // 2)
-        for w in range(2):
-            for g in range(NPASS):
-                mm_phi(3, w, g)
+        theta_turn(2)
+        phi_turn(2)
         g_max(2, 1)
-        phi_add(2)
         g_first(3)
         theta_tanh(3, 0)
         theta_out(2)
+        phi_out(2)
         mm_g(3, 2, 0)
         quant(3, 1, CL // 2, CL)
         mm_g(3, 2, 1)
@@ -369,20 +380,19 @@ def tile_selfattention3d_pb_kernel(
         g_max(2, 2)
         mm_g(3, 3, 0)
         mm_g(3, 3, 1)
+        mm_phi(3)
         g_max(3, 1)
         g_max(2, 3)
         g_last(2)
-        for w in range(2, 4):
-            for g in range(NPASS):
-                mm_phi(3, w, g)
         theta_tanh(3, 1)
         g_max(3, 2)
         phi_pool(3)
-        phi_tanh(2)
-        theta_out(3)
-        g_max(3, 3)
-        phi_add(3)
+        theta_turn(3)
         phi_tanh(3)
+        phi_turn(3)
+        theta_out(3)
+        phi_out(3)
+        g_max(3, 3)
         for lo in (0, 256):
             g_bias(3, nc.vector, lo, lo + 256)
             g_store(3, lo, lo + 256)

@@ -20,8 +20,7 @@ NCHUNK = 4
 NPASS = 2
 CL = 512
 
-V_WIDEN = {(0, 0): 2, (0, 1): 1, (1, 0): 1}
-W_COPY_ON_SCALAR = (True, True, True, True, True, True)
+V_WIDEN = {(0, 0): 2, (0, 1): 1}
 G_BIAS = (2,)
 
 
@@ -80,6 +79,7 @@ def tile_selfattention3d_pb_kernel(
         ident = keep.tile([P, P], F32, name="ident", tag="ident")
         make_identity(nc, ident[:])
 
+        plain = {}
         wide = {}
         grp = {}
         xc = {}
@@ -98,6 +98,21 @@ def tile_selfattention3d_pb_kernel(
                     )
                 else:
                     nc.scalar.activation(out=wd[:, t, :], in_=src[:, t, :].bitcast(FP8), func=ACT.Copy, scale=col)
+
+        def cast(c, g):
+            plain[(c, g)] = work.tile([P, 4, CL], BF16, name="plain_%d_%d" % (c, g), tag="plain", bufs=2)
+            nc.scalar.copy(
+                out=plain[(c, g)][:].rearrange("p t n -> p (t n)"),
+                in_=xbytes[(c, g)][:].rearrange("p t n -> p (t n)").bitcast(FP8),
+            )
+
+        def scale(c, g):
+            wide[(c, g)] = work.tile([P, 4, CL], BF16, name="wide_%d_%d" % (c, g), tag="wide", bufs=4)
+            for t in range(4):
+                nc.vector.tensor_scalar(
+                    out=wide[(c, g)][:, t, :], in0=plain[(c, g)][:, t, :],
+                    scalar1=xsc[:, 4 * g + t:4 * g + t + 1], scalar2=None, op0=ALU.mult,
+                )
 
         def inter_half(c, g, di, on_scalar=False):
             if di == 0:
@@ -131,19 +146,19 @@ def tile_selfattention3d_pb_kernel(
             wc.append(keep.tile([P, 768], U32, name="wc%d" % g, tag="wc%d" % g, align_bytes=64))
             wsc.append(keep.tile([P, 768], U8, name="wsc%d" % g, tag="wsc%d" % g, align_bytes=64))
 
-        def wprep(q, g):
-            bank = psum.tile([P, 2, 2, P], F32, name="wt_%d_%d" % (q, g), tag="G", bufs=5)
+        wbank = {}
+
+        def w_turn(q, g):
+            wbank[(q, g)] = psum.tile([P, 2, 2, P], F32, name="wt_%d_%d" % (q, g), tag="G", bufs=5)
             for r in range(2):
                 words = wraw[2 * q + r][:].bitcast(F32)
                 for u in range(2):
-                    nc.tensor.transpose(bank[:, r, u, :], words[:, 256 * g + u:256 * (g + 1):2], ident[:])
+                    nc.tensor.transpose(wbank[(q, g)][:, r, u, :], words[:, 256 * g + u:256 * (g + 1):2], ident[:])
+
+        def w_copy(q, g):
             dst = wgrp[g][:].rearrange("p o t -> p (o t)").bitcast(F32)[:, 512 * q:512 * (q + 1)]
             dst = dst.rearrange("p (r o u) -> p r o u", r=2, o=P, u=2)
-            src = bank[:].rearrange("p r u o -> p r o u")
-            if W_COPY_ON_SCALAR[2 * q + g]:
-                nc.scalar.copy(out=dst, in_=src)
-            else:
-                nc.vector.tensor_copy(out=dst, in_=src)
+            nc.scalar.copy(out=dst, in_=wbank[(q, g)][:].rearrange("p r u o -> p r o u"))
 
         def wquant(g, lo, hi):
             flat = wgrp[g][:].rearrange("p o t -> p (o t)")
@@ -267,37 +282,45 @@ def tile_selfattention3d_pb_kernel(
         widen(0, 0)
         widen(0, 1)
         inter(0, 0)
-        wprep(0, 0)
-        wprep(0, 1)
+        for g in range(NPASS):
+            w_turn(0, g)
+        cast(1, 0)
+        for g in range(NPASS):
+            w_copy(0, g)
         inter_half(0, 1, 0)
         quant(0, 0)
         inter_half(0, 1, 1)
-        widen(1, 0, (0, 1, 2))
-        wprep(1, 0)
-        wprep(1, 1)
+        scale(1, 0)
         quant(0, 1)
-        widen(1, 0, (3,))
+        for g in range(NPASS):
+            w_turn(1, g)
+        for g in range(NPASS):
+            w_copy(1, g)
+        inter_half(1, 0, 0)
         wquant(0, 0, 256)
         wquant(1, 0, 256)
-        wprep(2, 0)
-        wprep(2, 1)
-        inter_half(1, 0, 0)
-        widen(1, 1)
-        wquant(0, 256, 768)
-        wquant(1, 256, 768)
         inter_half(1, 0, 1)
+        for g in range(NPASS):
+            w_turn(2, g)
+        cast(1, 1)
+        for g in range(NPASS):
+            w_copy(2, g)
+        scale(1, 1)
+        wquant(0, 256, 768)
+        quant(1, 0)
+        wquant(1, 256, 768)
         widen(2, 0)
         for g in range(NPASS):
             mm_theta(0, g)
+        mm_phi(0)
         for w in range(4):
             mm_window(0, w)
-        mm_phi(0)
-        quant(1, 0)
         inter_half(1, 1, 0)
         inter_half(1, 1, 1)
         phi_pool(0)
         quant(1, 1)
 
+        widen(2, 1, (0,))
         g_first(0)
         theta_tanh(0, 0)
         theta_tanh(0, 1)
@@ -308,7 +331,7 @@ def tile_selfattention3d_pb_kernel(
         phi_turn(0)
         for g in range(NPASS):
             mm_theta(1, g)
-        widen(2, 1)
+        widen(2, 1, (1, 2, 3))
         theta_out(0)
         phi_out(0)
         widen(3, 0)

@@ -60,15 +60,16 @@ def tile_selfattention3d_pb_kernel(
         load_x(1, 1)
         nc.sync.dma_start(out=wraw[4][:], in_=wg_rows[2])
         nc.sync.dma_start(out=wraw[5][:], in_=wg_rows[3])
+        load_x(2, 0)
+        load_x(2, 1)
         bth = keep.tile([P, 1], BF16, name="bth", tag="bth")
         nc.sync.dma_start(out=bth[:], in_=b_theta.rearrange("(p o) -> p o", o=1))
         bphi = keep.tile([P, 1], BF16, name="bphi", tag="bphi")
         nc.sync.dma_start(out=bphi[:], in_=b_phi.rearrange("(p o) -> p o", o=1))
+        load_x(3, 0)
+        load_x(3, 1)
         bg = keep.tile([P, 512], BF16, name="bg", tag="bg")
         nc.sync.dma_start(out=bg[:], in_=b_g.partition_broadcast(P))
-        for c in range(2, NCHUNK):
-            for g in range(NPASS):
-                load_x(c, g)
 
 
         warm = keep.tile([P, 1], F32, name="warm", tag="warm")
@@ -248,10 +249,14 @@ def tile_selfattention3d_pb_kernel(
             turned[c] = psum.tile([P, P], F32, name="FT_%d" % c, tag="F", bufs=1)
             nc.tensor.transpose(turned[c][:], ph[c][:], ident[:])
 
+        phi_rows = {}
+
         def phi_out(c):
-            po = work.tile([P, P], F32, name="po_%d" % c, tag="po", bufs=2)
-            nc.scalar.copy(out=po[:], in_=turned[c][:])
-            nc.sync.dma_start(out=out_1[0, P * c:P * (c + 1), :], in_=po[:])
+            phi_rows[c] = work.tile([P, P], F32, name="po_%d" % c, tag="po", bufs=2)
+            nc.scalar.copy(out=phi_rows[c][:], in_=turned[c][:])
+
+        def phi_store(c):
+            nc.sync.dma_start(out=out_1[0, P * c:P * (c + 1), :], in_=phi_rows[c][:])
 
         th = {}
 
@@ -334,6 +339,7 @@ def tile_selfattention3d_pb_kernel(
         widen(2, 1, (1, 2, 3))
         theta_out(0)
         phi_out(0)
+        phi_store(0)
         widen(3, 0)
         inter_half(2, 0, 0)
         g_max(0, 1)
@@ -361,6 +367,7 @@ def tile_selfattention3d_pb_kernel(
         widen(3, 1)
         theta_out(1)
         phi_out(1)
+        phi_store(1)
         inter_half(3, 0, 0)
         for g in range(NPASS):
             mm_theta(2, g)
@@ -395,6 +402,7 @@ def tile_selfattention3d_pb_kernel(
         theta_tanh(3, 0)
         theta_out(2)
         phi_out(2)
+        phi_store(2)
         mm_g(3, 2, 0)
         quant(3, 1, CL // 2, CL)
         mm_g(3, 2, 1)
@@ -411,11 +419,12 @@ def tile_selfattention3d_pb_kernel(
         g_max(3, 2)
         phi_pool(3)
         theta_turn(3)
+        theta_out(3)
         phi_tanh(3)
         phi_turn(3)
-        theta_out(3)
         phi_out(3)
         g_max(3, 3)
         for lo in (0, 256):
             g_bias(3, nc.vector, lo, lo + 256)
             g_store(3, lo, lo + 256)
+        phi_store(3)

from contextlib import ExitStack

import concourse.mybir as mybir
from concourse.masks import make_identity

FLOPS = 2 * 1024 * 768 * 2048

F32 = mybir.dt.float32
BF16 = mybir.dt.bfloat16
U32 = mybir.dt.uint32
U8 = mybir.dt.uint8
FP8 = mybir.dt.float8_e4m3fn
FP8X4 = mybir.dt.float8_e4m3fn_x4
ACT = mybir.ActivationFunctionType
ALU = mybir.AluOpType
AX = mybir.AxisListType

P = 128
NCHUNK = 4
NPASS = 2
CL = 512

V_WIDEN = {(0, 0): 2, (0, 1): 1}
G_BIAS = (2,)


def tile_selfattention3d_pb_kernel(
    tc, x_bytes, x_scale, w_theta, b_theta, w_phi, b_phi, w_g, b_g, out_0, out_1, out_2
):
    nc = tc.nc
    with ExitStack() as ctx:
        keep = ctx.enter_context(tc.tile_pool(name="keep", bufs=1))
        work = ctx.enter_context(tc.tile_pool(name="work", bufs=2))
        psum = ctx.enter_context(tc.psum_pool(name="psum", bufs=1))

        xsc = keep.tile([P, 8], F32, name="xsc", tag="xsc")
        nc.sync.dma_start(
            out=xsc[:].rearrange("p (g t) -> p g t", g=NPASS),
            in_=x_scale.rearrange("o k a b c -> (o k a b c)").rearrange("(g p t) -> p g t", g=NPASS, p=P, t=4),
        )
        xb = x_bytes[0].rearrange("(g p t) f i j -> g p t (f i j)", g=NPASS, p=P, t=4)
        xbytes = {}

        def load_x(c, g):
            xbytes[(c, g)] = keep.tile([P, 4, CL], U8, name="xbytes_%d_%d" % (c, g), tag="xbytes_%d_%d" % (c, g))
            nc.sync.dma_start(out=xbytes[(c, g)][:], in_=xb[g][:, :, c * CL:(c + 1) * CL])

        wraw = []
        for r in range(6):
            wraw.append(keep.tile([P, 1024], BF16, name="wraw%d" % r, tag="wraw%d" % r))
        wg_rows = w_g.rearrange("(r p) k -> r p k", p=P)

        load_x(0, 0)
        load_x(0, 1)
        nc.sync.dma_start(out=wraw[0][:], in_=w_theta)
        nc.sync.dma_start(out=wraw[1][:], in_=w_phi)
        load_x(1, 0)
        nc.sync.dma_start(out=wraw[2][:], in_=wg_rows[0])
        nc.sync.dma_start(out=wraw[3][:], in_=wg_rows[1])
        load_x(1, 1)
        nc.sync.dma_start(out=wraw[4][:], in_=wg_rows[2])
        nc.sync.dma_start(out=wraw[5][:], in_=wg_rows[3])
        load_x(2, 0)
        load_x(2, 1)
        bth = keep.tile([P, 1], BF16, name="bth", tag="bth")
        nc.sync.dma_start(out=bth[:], in_=b_theta.rearrange("(p o) -> p o", o=1))
        bphi = keep.tile([P, 1], BF16, name="bphi", tag="bphi")
        nc.sync.dma_start(out=bphi[:], in_=b_phi.rearrange("(p o) -> p o", o=1))
        load_x(3, 0)
        load_x(3, 1)
        bg = keep.tile([P, 512], BF16, name="bg", tag="bg")
        nc.sync.dma_start(out=bg[:], in_=b_g.partition_broadcast(P))


        warm = keep.tile([P, 1], F32, name="warm", tag="warm")
        nc.vector.memset(warm[:], 0.0)
        warm2 = keep.tile([P, 1], F32, name="warm2", tag="warm2")
        nc.scalar.activation(out=warm2[:], in_=warm[:], func=ACT.Tanh)

        ident = keep.tile([P, P], F32, name="ident", tag="ident")
        make_identity(nc, ident[:])

        plain = {}
        wide = {}
        grp = {}
        xc = {}
        xs = {}

        def widen(c, g, planes=(0, 1, 2, 3)):
            if (c, g) not in wide:
                wide[(c, g)] = work.tile([P, 4, CL], BF16, name="wide_%d_%d" % (c, g), tag="wide", bufs=4)
            wd = wide[(c, g)]
            src = xbytes[(c, g)]
            for t in planes:
                col = xsc[:, 4 * g + t:4 * g + t + 1]
                if t < V_WIDEN.get((c, g), 0):
                    nc.vector.tensor_scalar(
                        out=wd[:, t, :], in0=src[:, t, :].bitcast(FP8), scalar1=col, scalar2=None, op0=ALU.mult
                    )
                else:
                    nc.scalar.activation(out=wd[:, t, :], in_=src[:, t, :].bitcast(FP8), func=ACT.Copy, scale=col)

        def cast(c, g):
            plain[(c, g)] = work.tile([P, 4, CL], BF16, name="plain_%d_%d" % (c, g), tag="plain", bufs=2)
            nc.scalar.copy(
                out=plain[(c, g)][:].rearrange("p t n -> p (t n)"),
                in_=xbytes[(c, g)][:].rearrange("p t n -> p (t n)").bitcast(FP8),
            )

        def scale(c, g):
            wide[(c, g)] = work.tile([P, 4, CL], BF16, name="wide_%d_%d" % (c, g), tag="wide", bufs=4)
            for t in range(4):
                nc.vector.tensor_scalar(
                    out=wide[(c, g)][:, t, :], in0=plain[(c, g)][:, t, :],
                    scalar1=xsc[:, 4 * g + t:4 * g + t + 1], scalar2=None, op0=ALU.mult,
                )

        def inter_half(c, g, di, on_scalar=False):
            if di == 0:
                grp[(c, g)] = work.tile([P, CL, 4], BF16, name="grp_%d_%d" % (c, g), tag="grp", bufs=3, align_bytes=64)
            gr = grp[(c, g)]
            src = wide[(c, g)][:].rearrange("p t (a di j b dj) -> p di a j t b dj", a=16, di=2, j=4, b=2, dj=2)
            dst = gr[:].rearrange("p (di dj a j b) t -> p di a j t b dj", di=2, dj=2, a=16, j=4, b=2)
            if on_scalar:
                nc.scalar.copy(out=dst[:, di], in_=src[:, di])
            else:
                nc.vector.tensor_copy(out=dst[:, di], in_=src[:, di])

        def inter(c, g):
            for di in range(2):
                inter_half(c, g, di)

        def quant(c, g, lo=0, hi=CL):
            if lo == 0:
                xc[(c, g)] = keep.tile([P, CL], U32, name="xc_%d_%d" % (c, g), tag="xc_%d_%d" % (c, g), align_bytes=64)
                xs[(c, g)] = keep.tile([P, CL], U8, name="xs_%d_%d" % (c, g), tag="xs_%d_%d" % (c, g), align_bytes=64)
            flat = grp[(c, g)][:].rearrange("p n t -> p (n t)")
            nc.vector.quantize_mx(
                out=xc[(c, g)][:, lo:hi].bitcast(FP8X4), scales=xs[(c, g)][:, lo:hi], in_=flat[:, 4 * lo:4 * hi]
            )

        wgrp = []
        wc = []
        wsc = []
        for g in range(NPASS):
            wgrp.append(keep.tile([P, 768, 4], BF16, name="wgrp%d" % g, tag="wgrp%d" % g, align_bytes=64))
            wc.append(keep.tile([P, 768], U32, name="wc%d" % g, tag="wc%d" % g, align_bytes=64))
            wsc.append(keep.tile([P, 768], U8, name="wsc%d" % g, tag="wsc%d" % g, align_bytes=64))

        wbank = {}

        def w_turn(q, g):
            wbank[(q, g)] = psum.tile([P, 2, 2, P], F32, name="wt_%d_%d" % (q, g), tag="G", bufs=5)
            for r in range(2):
                words = wraw[2 * q + r][:].bitcast(F32)
                for u in range(2):
                    nc.tensor.transpose(wbank[(q, g)][:, r, u, :], words[:, 256 * g + u:256 * (g + 1):2], ident[:])

        def w_copy(q, g):
            dst = wgrp[g][:].rearrange("p o t -> p (o t)").bitcast(F32)[:, 512 * q:512 * (q + 1)]
            dst = dst.rearrange("p (r o u) -> p r o u", r=2, o=P, u=2)
            nc.scalar.copy(out=dst, in_=wbank[(q, g)][:].rearrange("p r u o -> p r o u"))

        def wquant(g, lo, hi):
            flat = wgrp[g][:].rearrange("p o t -> p (o t)")
            nc.vector.quantize_mx(
                out=wc[g][:, lo:hi].bitcast(FP8X4), scales=wsc[g][:, lo:hi], in_=flat[:, 4 * lo:4 * hi]
            )

        tbank = {}
        fbank = {}
        gbank = {}

        def mm_theta(c, g, lo=0, hi=CL):
            if lo == 0 and g == 0:
                tbank[c] = psum.tile([P, CL], F32, name="T_%d" % c, tag="T", bufs=1)
            nc.tensor.matmul_mx(
                out=tbank[c][:, lo:hi],
                lhsT=wc[g][:, 0:128].bitcast(FP8X4), lhsT_scale=wsc[g][:, 0:128],
                rhs=xc[(c, g)][:, lo:hi].bitcast(FP8X4), rhs_scale=xs[(c, g)][:, lo:hi],
                start=(g == 0), stop=(g == NPASS - 1),
            )

        def mm_g(c, w, g):
            if g == 0:
                gbank[(c, w)] = psum.tile([P, 512], F32, name="G_%d_%d" % (c, w), tag="G", bufs=5)
            cols = slice(P * w, P * (w + 1))
            nc.tensor.matmul_mx(
                out=gbank[(c, w)][:],
                lhsT=xc[(c, g)][:, cols].bitcast(FP8X4), lhsT_scale=xs[(c, g)][:, cols],
                rhs=wc[g][:, 256:768].bitcast(FP8X4), rhs_scale=wsc[g][:, 256:768],
                start=(g == 0), stop=(g == NPASS - 1),
            )

        def mm_phi(c):
            fbank[c] = psum.tile([P, CL], F32, name="F_%d" % c, tag="F", bufs=1)
            for g in range(NPASS):
                nc.tensor.matmul_mx(
                    out=fbank[c][:],
                    lhsT=wc[g][:, 128:256].bitcast(FP8X4), lhsT_scale=wsc[g][:, 128:256],
                    rhs=xc[(c, g)][:].bitcast(FP8X4), rhs_scale=xs[(c, g)][:],
                    start=(g == 0), stop=(g == NPASS - 1),
                )

        def mm_window(c, w):
            for g in range(NPASS):
                mm_g(c, w, g)

        acc = {}

        def g_first(c):
            acc[c] = work.tile([P, 512], F32, name="acc_%d" % c, tag="acc", bufs=2)
            nc.scalar.copy(out=acc[c][:], in_=gbank[(c, 0)][:])

        def g_max(c, w):
            nc.vector.tensor_tensor(out=acc[c][:], in0=gbank[(c, w)][:], in1=acc[c][:], op=ALU.max)

        gout = {}

        def g_bias(c, engine, lo, hi):
            if lo == 0:
                gout[c] = work.tile([P, 512], F32, name="gout_%d" % c, tag="gout", bufs=2)
            engine.tensor_tensor(out=gout[c][:, lo:hi], in0=acc[c][:, lo:hi], in1=bg[:, lo:hi], op=ALU.add)

        def g_store(c, lo, hi):
            nc.sync.dma_start(out=out_2[0, P * c:P * (c + 1), lo:hi], in_=gout[c][:, lo:hi])

        def g_last(c):
            g_bias(c, nc.gpsimd if c in G_BIAS else nc.vector, 0, 512)
            g_store(c, 0, 512)

        pooled = {}

        def phi_pool(c):
            pooled[c] = work.tile([P, P], F32, name="pr_%d" % c, tag="pr", bufs=2)
            nc.vector.tensor_reduce(
                out=pooled[c][:], in_=fbank[c][:].rearrange("p (w m) -> p m w", w=4), axis=AX.X, op=ALU.max
            )

        ph = {}

        def phi_tanh(c):
            ph[c] = work.tile([P, P], F32, name="ph_%d" % c, tag="ph", bufs=2)
            nc.scalar.activation(out=ph[c][:], in_=pooled[c][:], func=ACT.Tanh, bias=bphi[:, 0:1])

        turned = {}

        def phi_turn(c):
            turned[c] = psum.tile([P, P], F32, name="FT_%d" % c, tag="F", bufs=1)
            nc.tensor.transpose(turned[c][:], ph[c][:], ident[:])

        phi_rows = {}

        def phi_out(c):
            phi_rows[c] = work.tile([P, P], F32, name="po_%d" % c, tag="po", bufs=2)
            nc.scalar.copy(out=phi_rows[c][:], in_=turned[c][:])

        def phi_store(c):
            nc.sync.dma_start(out=out_1[0, P * c:P * (c + 1), :], in_=phi_rows[c][:])

        th = {}

        def theta_tanh(c, di):
            if di == 0:
                th[c] = work.tile([P, CL], F32, name="th_%d" % c, tag="th", bufs=2)
            src = tbank[c][:].rearrange("p (di dj a j) -> p di dj a j", di=2, dj=2, a=16, j=8)
            dst = th[c][:].rearrange("p (dj a di j) -> p di dj a j", dj=2, a=16, di=2, j=8)
            nc.scalar.activation(out=dst[:, di], in_=src[:, di], func=ACT.Tanh, bias=bth[:, 0:1])

        out0v = out_0[0].rearrange("(c f p dj) k -> c p f (dj k)", c=NCHUNK, f=2, p=P, dj=2)

        ubank = {}

        def theta_turn(c):
            ubank[c] = psum.tile([P, 4, P], F32, name="U_%d" % c, tag="U", bufs=1)
            for dj in range(2):
                for f in range(2):
                    b = 2 * dj + f
                    nc.tensor.transpose(ubank[c][:, 2 * f + dj, :], th[c][:, P * b:P * (b + 1)], ident[:])

        def theta_out(c):
            to = work.tile([P, 4, P], F32, name="tho_%d" % c, tag="tho", bufs=2)
            nc.scalar.copy(out=to[:], in_=ubank[c][:])
            nc.sync.dma_start(out=out0v[c], in_=to[:].rearrange("p (f dj) k -> p f (dj k)", f=2))

        ctx.enter_context(tc.manual_schedule(engines={mybir.EngineType.DVE, mybir.EngineType.Activation, mybir.EngineType.PE}))
        widen(0, 0)
        widen(0, 1)
        inter(0, 0)
        for g in range(NPASS):
            w_turn(0, g)
        cast(1, 0)
        for g in range(NPASS):
            w_copy(0, g)
        inter_half(0, 1, 0)
        quant(0, 0)
        inter_half(0, 1, 1)
        scale(1, 0)
        quant(0, 1)
        for g in range(NPASS):
            w_turn(1, g)
        for g in range(NPASS):
            w_copy(1, g)
        inter_half(1, 0, 0)
        wquant(0, 0, 256)
        wquant(1, 0, 256)
        inter_half(1, 0, 1)
        for g in range(NPASS):
            w_turn(2, g)
        cast(1, 1)
        for g in range(NPASS):
            w_copy(2, g)
        scale(1, 1)
        wquant(0, 256, 768)
        quant(1, 0)
        wquant(1, 256, 768)
        widen(2, 0)
        for g in range(NPASS):
            mm_theta(0, g)
        mm_phi(0)
        for w in range(4):
            mm_window(0, w)
        inter_half(1, 1, 0)
        inter_half(1, 1, 1)
        phi_pool(0)
        quant(1, 1)

        widen(2, 1, (0,))
        g_first(0)
        theta_tanh(0, 0)
        theta_tanh(0, 1)
        phi_tanh(0)
        mm_window(1, 0)
        mm_window(1, 1)
        theta_turn(0)
        phi_turn(0)
        for g in range(NPASS):
            mm_theta(1, g)
        widen(2, 1, (1, 2, 3))
        theta_out(0)
        phi_out(0)
        phi_store(0)
        widen(3, 0)
        inter_half(2, 0, 0)
        g_max(0, 1)
        inter_half(2, 0, 1)
        g_max(0, 2)
        quant(2, 0)
        g_max(0, 3)
        mm_window(1, 2)
        mm_window(1, 3)
        mm_phi(1)
        inter_half(2, 1, 0)
        g_last(0)
        inter_half(2, 1, 1)
        phi_pool(1)

        g_first(1)
        theta_tanh(1, 0)
        theta_tanh(1, 1)
        phi_tanh(1)
        quant(2, 1)
        mm_window(2, 0)
        mm_window(2, 1)
        theta_turn(1)
        phi_turn(1)
        widen(3, 1)
        theta_out(1)
        phi_out(1)
        phi_store(1)
        inter_half(3, 0, 0)
        for g in range(NPASS):
            mm_theta(2, g)
        g_max(1, 1)
        inter_half(3, 0, 1)
        g_max(1, 2)
        mm_window(2, 2)
        mm_window(2, 3)
        mm_phi(2)
        quant(3, 0)
        g_first(2)
        theta_tanh(2, 0)
        theta_tanh(2, 1)
        inter_half(3, 1, 0)
        inter_half(3, 1, 1, on_scalar=True)
        g_max(1, 3)
        mm_g(3, 0, 0)
        mm_g(3, 1, 0)
        quant(3, 1, 0, CL // 2)
        g_last(1)
        mm_g(3, 0, 1)
        mm_g(3, 1, 1)

        phi_pool(2)
        phi_tanh(2)
        for g in range(NPASS):
            mm_theta(3, g, 0, CL // 2)
        theta_turn(2)
        phi_turn(2)
        g_max(2, 1)
        g_first(3)
        theta_tanh(3, 0)
        theta_out(2)
        phi_out(2)
        phi_store(2)
        mm_g(3, 2, 0)
        quant(3, 1, CL // 2, CL)
        mm_g(3, 2, 1)
        for g in range(NPASS):
            mm_theta(3, g, CL // 2, CL)
        g_max(2, 2)
        mm_g(3, 3, 0)
        mm_g(3, 3, 1)
        mm_phi(3)
        g_max(3, 1)
        g_max(2, 3)
        g_last(2)
        theta_tanh(3, 1)
        g_max(3, 2)
        phi_pool(3)
        theta_turn(3)
        theta_out(3)
        phi_tanh(3)
        phi_turn(3)
        phi_out(3)
        g_max(3, 3)
        for lo in (0, 256):
            g_bias(3, nc.vector, lo, lo + 256)
            g_store(3, lo, lo + 256)
        phi_store(3)
